import numpy as np
import ml_dtypes


def mxq(x, axis, fmt="e4m3"):
    dtype, down = {"e4m3": (ml_dtypes.float8_e4m3fn, 7), "e5m2": (ml_dtypes.float8_e5m2, 14)}[fmt]
    v = np.moveaxis(np.asarray(x, np.float32).astype(ml_dtypes.bfloat16).astype(np.float64), axis, -1)
    blocks = v.reshape(v.shape[:-1] + (-1, 32))
    amax = np.abs(blocks).max(-1, keepdims=True)
    byte = np.maximum(np.where(amax > 0, np.frexp(amax)[1] - 1 + 127, 0) - down, 1)
    scale = np.exp2(byte - 127.0)
    codes = (blocks / scale).astype(np.float32).astype(dtype).astype(np.float64)
    return np.moveaxis((codes * scale).reshape(v.shape), -1, axis)


WIDE = False


def mx_kscale(k):
    if not WIDE:
        return np.ones(k)
    levels = np.array([10, -10, 5, -5, 0])
    a = np.random.permutation(np.resize(levels, k // 512 * 4)).reshape(k // 512, 4)
    idx = np.arange(k)
    return np.exp2(a[idx // 512, idx % 128 // 32])


BF16 = ml_dtypes.bfloat16


def bf(x):
    return np.asarray(x, np.float32).astype(BF16)


def f64(x):
    return np.asarray(x).astype(np.float64)


B, DIM, E, HID = 1024, 1024, 1024, 2048
EPS = 1e-5


def layer_norm(y, g, b):
    m = y.mean(-1, keepdims=True)
    v = ((y - m) ** 2).mean(-1, keepdims=True)
    return (y - m) / np.sqrt(v + EPS) * g + b


def setup_inputs():
    t = mx_kscale(E)
    r = np.random.standard_normal
    return {'feat': bf(r((B, DIM))),
            'Wv': bf(r((E, DIM)) / np.sqrt(DIM) * t[:, None]),
            'bv': bf(r(E) * 0.2 * t),
            'Wo': bf(r((DIM, E)) / np.sqrt(E) / t[None, :]),
            'bo': bf(r(DIM) * 0.2),
            'g': bf(1.0 + 0.1 * r(DIM)),
            'be': bf(0.1 * r(DIM))}


def reference(feat, Wv, bv, Wo, bo, g, be):
    x = f64(feat)
    val = (mxq(x, 1, 'e4m3') @ mxq(f64(Wv), 1, 'e4m3').T) + f64(bv)
    att = (mxq(val, 1, 'e4m3') @ mxq(f64(Wo), 1, 'e4m3').T) + f64(bo)
    return layer_norm(x + att, f64(g), f64(be))

@@ -1,0 +1,238 @@
+from contextlib import ExitStack
+
+import concourse.mybir as mybir
+from concourse.masks import make_identity
+
+F32 = mybir.dt.float32
+BF16 = mybir.dt.bfloat16
+U32 = mybir.dt.uint32
+U8 = mybir.dt.uint8
+FP8X4 = mybir.dt.float8_e4m3fn_x4
+ACT = mybir.ActivationFunctionType
+ALU = mybir.AluOpType
+
+P = 128
+PACK = 4
+SIZE = 1024
+PASSES = SIZE // (P * PACK)
+TILES = SIZE // P
+PAIR = 2 * P
+PAIRS = SIZE // PAIR
+ROW_WORDS = SIZE // 2
+BANK = 512
+HALVES = SIZE // BANK
+EPS = 1e-5
+
+FLOPS = 2 * 2 * SIZE * SIZE * SIZE
+
+
+def quantise_pair(nc, stage, psum_flip, identity, words, codes, scales):
+    grouped = stage.tile([P, PASSES * PAIR * PACK], BF16, align_bytes=64)
+    grouped_words = grouped[:].bitcast(F32).rearrange("p (c n u) -> p c n u", c=PASSES, u=2)
+    for i in range(2):
+        flipped = psum_flip.tile([P, 2 * PASSES, P], F32, tag="flip")
+        for block in range(2 * PASSES):
+            first = (i * 2 * PASSES + block) * P
+            nc.tensor.transpose(flipped[:, block, :], words[:, first : first + P], identity)
+        copy_out = (nc.scalar.copy, nc.vector.tensor_copy)[i]
+        copy_out(
+            out=grouped_words[:, :, i * P : (i + 1) * P, :],
+            in_=flipped[:].rearrange("p (c u) r -> p c r u", u=2),
+        )
+    width = PAIR * PACK
+    for c in range(PASSES):
+        nc.vector.quantize_mx(
+            out=codes[:, c, :].bitcast(FP8X4),
+            scales=scales[:, c, :],
+            in_=grouped[:, c * width : (c + 1) * width],
+        )
+
+
+def tile_efficientfusionlayer_pa_kernel(tc, feat, w_val, b_val, w_out, b_out, gain, shift, out):
+    nc = tc.nc
+    with ExitStack() as ctx:
+        keep = ctx.enter_context(tc.tile_pool(name="keep", bufs=1))
+        stage = ctx.enter_context(tc.tile_pool(name="stage", bufs=3))
+        rows = ctx.enter_context(tc.tile_pool(name="rows", bufs=3))
+        stats = ctx.enter_context(tc.tile_pool(name="stats", bufs=4))
+        psum_flip = ctx.enter_context(tc.psum_pool(name="psum_flip", bufs=2))
+        psum_val = ctx.enter_context(tc.psum_pool(name="psum_val", bufs=2))
+        psum_att = ctx.enter_context(tc.psum_pool(name="psum_att", bufs=4))
+
+        vectors = keep.tile([P, 3 * SIZE], BF16)
+        nc.vector.memset(vectors[:], 0.0)
+        for v, vector in enumerate((b_out, gain, shift)):
+            nc.scalar.dma_start(
+                out=vectors[0:1, v * SIZE : (v + 1) * SIZE], in_=vector.rearrange("(o d) -> o d", o=1)
+            )
+        bias_bf = keep.tile([P, TILES], BF16)
+        with nc.allow_non_contiguous_dma(reason="1024 bias values, two to a piece"):
+            nc.scalar.dma_start(
+                out=bias_bf[:].rearrange("p (r e) -> p r e", e=2),
+                in_=b_val.rearrange("(r p e) -> p r e", p=P, e=2),
+            )
+
+        wv_sb = keep.tile([P, TILES * SIZE], BF16)
+        wv_rows = w_val.rearrange("(r p e) d -> p r (e d)", p=P, e=2)
+        feat_sb = keep.tile([P, TILES * SIZE], BF16)
+        feat_rows = feat.rearrange("(p j) d -> p (j d)", j=TILES)
+        wo_sb = keep.tile([P, TILES * SIZE], BF16)
+        wo_rows = w_out.rearrange("(i p) k -> p i k", p=P)
+        span = 2 * SIZE
+        for r in range(PAIRS):
+            nc.sync.dma_start(out=wv_sb[:, r * span : (r + 1) * span], in_=wv_rows[:, r, :])
+        for r in range(PAIRS):
+            nc.sync.dma_start(out=feat_sb[:, r * span : (r + 1) * span], in_=feat_rows[:, r * span : (r + 1) * span])
+        for r in range(PAIRS):
+            nc.sync.dma_start(
+                out=wo_sb[:, r * span : (r + 1) * span].rearrange("p (i k) -> p i k", i=2),
+                in_=wo_rows[:, 2 * r : 2 * r + 2, :],
+            )
+
+        identity = keep.tile([P, P], F32)
+        make_identity(nc, identity[:])
+        ones = keep.tile([P, P], BF16)
+        nc.vector.memset(ones[:], 1.0)
+        eps = keep.tile([P, 1], F32)
+        nc.vector.memset(eps[:], EPS)
+        warm = keep.tile([P, 1], F32)
+        nc.scalar.activation(out=warm[:], in_=eps[:], func=ACT.Sqrt)
+        bias_val = keep.tile([P, TILES], F32)
+        nc.vector.tensor_copy(out=bias_val[:], in_=bias_bf[:])
+
+        codes = {}
+        scales = {}
+        for name in ("wv", "feat", "wo", "val"):
+            codes[name] = keep.tile([P, PASSES, SIZE], U32, name="codes_" + name, align_bytes=64)
+            scales[name] = keep.tile([P, PASSES, SIZE], U8, name="scales_" + name, align_bytes=64)
+
+        def quantise_matrix(name, raw):
+            words = raw[:].bitcast(F32)
+            for r in range(PAIRS):
+                quantise_pair(
+                    nc, stage, psum_flip, identity[:],
+                    words[:, r * 2 * ROW_WORDS : (r + 1) * 2 * ROW_WORDS],
+                    codes[name][:, :, r * PAIR : (r + 1) * PAIR],
+                    scales[name][:, :, r * PAIR : (r + 1) * PAIR],
+                )
+
+        def value_layer(r, c):
+            cols = slice(r * PAIR, (r + 1) * PAIR)
+            planes = stage.tile([P, PACK, PAIR], BF16)
+            for t in range(0, PACK, 2):
+                acc = psum_val.tile([P, 2, PAIR], F32)
+                for i in range(2):
+                    m = c * PACK + t + i
+                    for d in range(PASSES):
+                        nc.tensor.matmul_mx(
+                            out=acc[:, i, :],
+                            lhsT=codes["wv"][:, d, m * P : (m + 1) * P].bitcast(FP8X4),
+                            lhsT_scale=scales["wv"][:, d, m * P : (m + 1) * P],
+                            rhs=codes["feat"][:, d, cols].bitcast(FP8X4),
+                            rhs_scale=scales["feat"][:, d, cols],
+                            start=(d == 0),
+                            stop=(d == PASSES - 1),
+                        )
+                for i in range(2):
+                    m = c * PACK + t + i
+                    nc.scalar.activation(
+                        out=planes[:, t + i, :], in_=acc[:, i, :], func=ACT.Identity,
+                        bias=bias_val[:, m : m + 1], scale=1.0,
+                    )
+            packed = stage.tile([P, PAIR * PACK], BF16, align_bytes=64)
+            nc.scalar.copy(
+                out=packed[:].rearrange("p (n i t) -> p n t i", i=4, t=PACK),
+                in_=planes[:].rearrange("p t (n i) -> p n t i", i=4),
+            )
+            nc.vector.quantize_mx(
+                out=codes["val"][:, c, cols].bitcast(FP8X4), scales=scales["val"][:, c, cols], in_=packed[:]
+            )
+
+        def centre_rows(j):
+            cols = slice(j * P, (j + 1) * P)
+            y = rows.tile([P, SIZE], F32)
+            sums = stats.tile([P, HALVES], F32)
+            for h in range(HALVES):
+                acc = psum_att.tile([P, BANK], F32)
+                for c in range(PASSES):
+                    nc.tensor.matmul_mx(
+                        out=acc[:],
+                        lhsT=codes["val"][:, c, cols].bitcast(FP8X4),
+                        lhsT_scale=scales["val"][:, c, cols],
+                        rhs=codes["wo"][:, c, h * BANK : (h + 1) * BANK].bitcast(FP8X4),
+                        rhs_scale=scales["wo"][:, c, h * BANK : (h + 1) * BANK],
+                        start=(c == 0),
+                        stop=(c == PASSES - 1),
+                    )
+                nc.vector.scalar_tensor_tensor(
+                    out=y[:, h * BANK : (h + 1) * BANK], in0=acc[:], scalar=1.0,
+                    in1=residual[:, j * SIZE + h * BANK : j * SIZE + (h + 1) * BANK],
+                    op0=ALU.mult, op1=ALU.add, accum_out=sums[:, h : h + 1],
+                )
+            minus_mean = stats.tile([P, 1], F32)
+            nc.vector.tensor_scalar(
+                out=minus_mean[:], in0=sums[:, 0:1], scalar1=sums[:, 1:2], scalar2=-1.0 / SIZE,
+                op0=ALU.add, op1=ALU.mult,
+            )
+            squares = rows.tile([P, SIZE], BF16)
+            sum_squares = stats.tile([P, 1], F32)
+            nc.scalar.activation(
+                out=squares[:], in_=y[:], func=ACT.Square, bias=minus_mean[:], scale=1.0,
+                accum_out=sum_squares[:],
+            )
+            deviation = stats.tile([P, 1], F32)
+            nc.scalar.activation(out=deviation[:], in_=sum_squares[:], func=ACT.Sqrt, bias=eps[:], scale=1.0 / SIZE)
+            centred = rows.tile([P, SIZE], F32)
+            nc.vector.scalar_tensor_tensor(
+                out=centred[:], in0=y[:], scalar=minus_mean[:], in1=gain_all, op0=ALU.add, op1=ALU.mult,
+            )
+            return centred, deviation
+
+        def finish_rows(j, centred, deviation):
+            inverse = stats.tile([P, 1], F32)
+            nc.vector.reciprocal(out=inverse[:], in_=deviation[:])
+            result = rows.tile([P, SIZE], F32)
+            nc.vector.scalar_tensor_tensor(
+                out=result[:], in0=centred[:], scalar=inverse[:], in1=shift_all, op0=ALU.mult, op1=ALU.add,
+            )
+            nc.sync.dma_start(out=out_rows[:, j, :], in_=result[:])
+
+        out_rows = out.rearrange("(p j) d -> p j d", j=TILES)
+
+        quantise_matrix("wv", wv_sb)
+
+        spread = keep.tile([P, 3 * SIZE], BF16)
+        for v in range(3):
+            copies = psum_flip.tile([P, SIZE], BF16, tag="flip")
+            for h in range(HALVES):
+                first = v * SIZE + h * BANK
+                nc.tensor.matmul(
+                    out=copies[:, h * BANK : (h + 1) * BANK], lhsT=ones[:], rhs=vectors[:, first : first + BANK],
+                    start=True, stop=True,
+                )
+            nc.scalar.copy(out=spread[:, v * SIZE : (v + 1) * SIZE], in_=copies[:])
+        b_out_all = spread[:, 0:SIZE]
+        gain_all = spread[:, SIZE : 2 * SIZE]
+        shift_all = spread[:, 2 * SIZE : 3 * SIZE]
+
+        quantise_matrix("feat", feat_sb)
+        residual = keep.tile([P, TILES * SIZE], F32)
+        for j in range(TILES):
+            nc.gpsimd.tensor_tensor(
+                out=residual[:, j * SIZE : (j + 1) * SIZE], in0=feat_sb[:, j * SIZE : (j + 1) * SIZE],
+                in1=b_out_all, op=ALU.add,
+            )
+        value_layer(0, 0)
+        value_layer(0, 1)
+        quantise_matrix("wo", wo_sb)
+
+        waiting = None
+        for j in range(TILES):
+            ahead = j + PASSES
+            if ahead < TILES:
+                value_layer(ahead // PASSES, ahead % PASSES)
+            centred, deviation = centre_rows(j)
+            if waiting is not None:
+                finish_rows(*waiting)
+            waiting = (j, centred, deviation)
+        finish_rows(*waiting)

@@ -18,7 +18,6 @@ PASSES = SIZE // (P * PACK)
 TILES = SIZE // P
 PAIR = 2 * P
 PAIRS = SIZE // PAIR
-ROW_WORDS = SIZE // 2
 BANK = 512
 HALVES = SIZE // BANK
 EPS = 1e-5
@@ -26,38 +25,17 @@ EPS = 1e-5
 FLOPS = 2 * 2 * SIZE * SIZE * SIZE
 
 
-def quantise_pair(nc, stage, psum_flip, identity, words, codes, scales):
-    grouped = stage.tile([P, PASSES * PAIR * PACK], BF16, align_bytes=64)
-    grouped_words = grouped[:].bitcast(F32).rearrange("p (c n u) -> p c n u", c=PASSES, u=2)
-    for i in range(2):
-        flipped = psum_flip.tile([P, 2 * PASSES, P], F32, tag="flip")
-        for block in range(2 * PASSES):
-            first = (i * 2 * PASSES + block) * P
-            nc.tensor.transpose(flipped[:, block, :], words[:, first : first + P], identity)
-        copy_out = (nc.scalar.copy, nc.vector.tensor_copy)[i]
-        copy_out(
-            out=grouped_words[:, :, i * P : (i + 1) * P, :],
-            in_=flipped[:].rearrange("p (c u) r -> p c r u", u=2),
-        )
-    width = PAIR * PACK
-    for c in range(PASSES):
-        nc.vector.quantize_mx(
-            out=codes[:, c, :].bitcast(FP8X4),
-            scales=scales[:, c, :],
-            in_=grouped[:, c * width : (c + 1) * width],
-        )
-
-
 def tile_efficientfusionlayer_pa_kernel(tc, feat, w_val, b_val, w_out, b_out, gain, shift, out):
     nc = tc.nc
     with ExitStack() as ctx:
         keep = ctx.enter_context(tc.tile_pool(name="keep", bufs=1))
         stage = ctx.enter_context(tc.tile_pool(name="stage", bufs=3))
-        rows = ctx.enter_context(tc.tile_pool(name="rows", bufs=3))
-        stats = ctx.enter_context(tc.tile_pool(name="stats", bufs=4))
-        psum_flip = ctx.enter_context(tc.psum_pool(name="psum_flip", bufs=2))
+        rows = ctx.enter_context(tc.tile_pool(name="rows", bufs=2))
+        stats = ctx.enter_context(tc.tile_pool(name="stats", bufs=3))
+        psum_keep = ctx.enter_context(tc.psum_pool(name="psum_keep", bufs=1))
+        psum_wide = ctx.enter_context(tc.psum_pool(name="psum_wide", bufs=4))
         psum_val = ctx.enter_context(tc.psum_pool(name="psum_val", bufs=2))
-        psum_att = ctx.enter_context(tc.psum_pool(name="psum_att", bufs=4))
+        ctx.enter_context(tc.manual_schedule())
 
         vectors = keep.tile([P, 3 * SIZE], BF16)
         nc.vector.memset(vectors[:], 0.0)
@@ -72,22 +50,23 @@ def tile_efficientfusionlayer_pa_kernel(tc, feat, w_val, b_val, w_out, b_out, ga
                 in_=b_val.rearrange("(r p e) -> p r e", p=P, e=2),
             )
 
-        wv_sb = keep.tile([P, TILES * SIZE], BF16)
-        wv_rows = w_val.rearrange("(r p e) d -> p r (e d)", p=P, e=2)
-        feat_sb = keep.tile([P, TILES * SIZE], BF16)
-        feat_rows = feat.rearrange("(p j) d -> p (j d)", j=TILES)
-        wo_sb = keep.tile([P, TILES * SIZE], BF16)
-        wo_rows = w_out.rearrange("(i p) k -> p i k", p=P)
         span = 2 * SIZE
+        raw = {}
+        for name in ("wv", "feat", "wo"):
+            raw[name] = keep.tile([P, TILES * SIZE], BF16, name="raw_" + name)
+        wv_rows = w_val.rearrange("(r p e) d -> p r (e d)", p=P, e=2)
         for r in range(PAIRS):
-            nc.sync.dma_start(out=wv_sb[:, r * span : (r + 1) * span], in_=wv_rows[:, r, :])
+            nc.sync.dma_start(out=raw["wv"][:, r * span : (r + 1) * span], in_=wv_rows[:, r, :])
+        feat_rows = feat.rearrange("(p j) d -> p (j d)", j=TILES)
         for r in range(PAIRS):
-            nc.sync.dma_start(out=feat_sb[:, r * span : (r + 1) * span], in_=feat_rows[:, r * span : (r + 1) * span])
+            nc.sync.dma_start(out=raw["feat"][:, r * span : (r + 1) * span], in_=feat_rows[:, r * span : (r + 1) * span])
+        wo_rows = w_out.rearrange("(i p) k -> p i k", p=P)
         for r in range(PAIRS):
             nc.sync.dma_start(
-                out=wo_sb[:, r * span : (r + 1) * span].rearrange("p (i k) -> p i k", i=2),
+                out=raw["wo"][:, r * span : (r + 1) * span].rearrange("p (i k) -> p i k", i=2),
                 in_=wo_rows[:, 2 * r : 2 * r + 2, :],
             )
+        out_rows = out.rearrange("(p j) d -> p j d", j=TILES)
 
         identity = keep.tile([P, P], F32)
         make_identity(nc, identity[:])
@@ -106,54 +85,104 @@ def tile_efficientfusionlayer_pa_kernel(tc, feat, w_val, b_val, w_out, b_out, ga
             codes[name] = keep.tile([P, PASSES, SIZE], U32, name="codes_" + name, align_bytes=64)
             scales[name] = keep.tile([P, PASSES, SIZE], U8, name="scales_" + name, align_bytes=64)
 
-        def quantise_matrix(name, raw):
-            words = raw[:].bitcast(F32)
-            for r in range(PAIRS):
-                quantise_pair(
-                    nc, stage, psum_flip, identity[:],
-                    words[:, r * 2 * ROW_WORDS : (r + 1) * 2 * ROW_WORDS],
-                    codes[name][:, :, r * PAIR : (r + 1) * PAIR],
-                    scales[name][:, :, r * PAIR : (r + 1) * PAIR],
+        pairs = [(name, r) for name in ("wv", "feat", "wo") for r in range(PAIRS)]
+        grouped_of = {}
+
+        def flip_pair(n):
+            name, r = pairs[n]
+            words = raw[name][:].bitcast(F32)
+            grouped = stage.tile([P, PASSES * PAIR * PACK], BF16, align_bytes=64)
+            grouped_words = grouped[:].bitcast(F32).rearrange("p (c n u) -> p c n u", c=PASSES, u=2)
+            for i in range(2):
+                flipped = psum_wide.tile([P, 2 * PASSES, P], F32, tag="wide")
+                for block in range(2 * PASSES):
+                    first = ((2 * r + i) * 2 * PASSES + block) * P
+                    nc.tensor.transpose(flipped[:, block, :], words[:, first : first + P], identity[:])
+                copy_out = (nc.scalar.copy, nc.vector.tensor_copy)[i]
+                copy_out(
+                    out=grouped_words[:, :, i * P : (i + 1) * P, :],
+                    in_=flipped[:].rearrange("p (c u) r -> p c r u", u=2),
+                )
+            grouped_of[n] = grouped
+
+        def quantise_pair(n):
+            name, r = pairs[n]
+            width = PAIR * PACK
+            for c in range(PASSES):
+                nc.vector.quantize_mx(
+                    out=codes[name][:, c, r * PAIR : (r + 1) * PAIR].bitcast(FP8X4),
+                    scales=scales[name][:, c, r * PAIR : (r + 1) * PAIR],
+                    in_=grouped_of[n][:, c * width : (c + 1) * width],
                 )
 
-        def value_layer(r, c):
-            cols = slice(r * PAIR, (r + 1) * PAIR)
-            planes = stage.tile([P, PACK, PAIR], BF16)
-            for t in range(0, PACK, 2):
+        val_acc = {}
+        planes_of = {}
+
+        def value_matmuls(h):
+            cols = slice((h // PASSES) * PAIR, (h // PASSES + 1) * PAIR)
+            for half in range(2):
                 acc = psum_val.tile([P, 2, PAIR], F32)
                 for i in range(2):
-                    m = c * PACK + t + i
-                    for d in range(PASSES):
+                    m = (h % PASSES) * PACK + 2 * half + i
+                    for c in range(PASSES):
                         nc.tensor.matmul_mx(
                             out=acc[:, i, :],
-                            lhsT=codes["wv"][:, d, m * P : (m + 1) * P].bitcast(FP8X4),
-                            lhsT_scale=scales["wv"][:, d, m * P : (m + 1) * P],
-                            rhs=codes["feat"][:, d, cols].bitcast(FP8X4),
-                            rhs_scale=scales["feat"][:, d, cols],
-                            start=(d == 0),
-                            stop=(d == PASSES - 1),
+                            lhsT=codes["wv"][:, c, m * P : (m + 1) * P].bitcast(FP8X4),
+                            lhsT_scale=scales["wv"][:, c, m * P : (m + 1) * P],
+                            rhs=codes["feat"][:, c, cols].bitcast(FP8X4),
+                            rhs_scale=scales["feat"][:, c, cols],
+                            start=(c == 0),
+                            stop=(c == PASSES - 1),
                         )
-                for i in range(2):
-                    m = c * PACK + t + i
-                    nc.scalar.activation(
-                        out=planes[:, t + i, :], in_=acc[:, i, :], func=ACT.Identity,
-                        bias=bias_val[:, m : m + 1], scale=1.0,
-                    )
+                val_acc[h, half] = acc
+
+        def value_bias(h, half):
+            if half == 0:
+                planes_of[h] = stage.tile([P, PACK, PAIR], BF16, name="planes")
+            for i in range(2):
+                t = 2 * half + i
+                m = (h % PASSES) * PACK + t
+                nc.scalar.activation(
+                    out=planes_of[h][:, t, :], in_=val_acc[h, half][:, i, :], func=ACT.Identity,
+                    bias=bias_val[:, m : m + 1], scale=1.0,
+                )
+
+        def value_quantise(h):
+            cols = slice((h // PASSES) * PAIR, (h // PASSES + 1) * PAIR)
             packed = stage.tile([P, PAIR * PACK], BF16, align_bytes=64)
             nc.scalar.copy(
                 out=packed[:].rearrange("p (n i t) -> p n t i", i=4, t=PACK),
-                in_=planes[:].rearrange("p t (n i) -> p n t i", i=4),
+                in_=planes_of[h][:].rearrange("p t (n i) -> p n t i", i=4),
             )
             nc.vector.quantize_mx(
-                out=codes["val"][:, c, cols].bitcast(FP8X4), scales=scales["val"][:, c, cols], in_=packed[:]
+                out=codes["val"][:, h % PASSES, cols].bitcast(FP8X4),
+                scales=scales["val"][:, h % PASSES, cols],
+                in_=packed[:],
             )
 
-        def centre_rows(j):
-            cols = slice(j * P, (j + 1) * P)
-            y = rows.tile([P, SIZE], F32)
-            sums = stats.tile([P, HALVES], F32)
+        att_acc = {}
+        residual_of = {}
+        y_of = {}
+        sums_of = {}
+        minus_mean_of = {}
+        sum_squares_of = {}
+        deviation_of = {}
+        inverse_of = {}
+        centred_of = {}
+
+        def add_b_out(j):
+            residual_of[j] = rows.tile([P, SIZE], F32, name="residual")
             for h in range(HALVES):
-                acc = psum_att.tile([P, BANK], F32)
+                nc.gpsimd.tensor_tensor(
+                    out=residual_of[j][:, h * BANK : (h + 1) * BANK],
+                    in0=raw["feat"][:, j * SIZE + h * BANK : j * SIZE + (h + 1) * BANK],
+                    in1=b_out_all[:, h * BANK : (h + 1) * BANK], op=ALU.add,
+                )
+
+        def output_matmuls(j):
+            cols = slice(j * P, (j + 1) * P)
+            for h in range(HALVES):
+                acc = psum_wide.tile([P, BANK], F32, tag="wide")
                 for c in range(PASSES):
                     nc.tensor.matmul_mx(
                         out=acc[:],
@@ -164,75 +193,110 @@ def tile_efficientfusionlayer_pa_kernel(tc, feat, w_val, b_val, w_out, b_out, ga
                         start=(c == 0),
                         stop=(c == PASSES - 1),
                     )
-                nc.vector.scalar_tensor_tensor(
-                    out=y[:, h * BANK : (h + 1) * BANK], in0=acc[:], scalar=1.0,
-                    in1=residual[:, j * SIZE + h * BANK : j * SIZE + (h + 1) * BANK],
-                    op0=ALU.mult, op1=ALU.add, accum_out=sums[:, h : h + 1],
-                )
-            minus_mean = stats.tile([P, 1], F32)
+                att_acc[j, h] = acc
+
+        def add_residual(j, h):
+            if h == 0:
+                y_of[j] = rows.tile([P, SIZE], F32, name="y")
+                sums_of[j] = stats.tile([P, HALVES], F32, name="sums")
+            nc.vector.scalar_tensor_tensor(
+                out=y_of[j][:, h * BANK : (h + 1) * BANK], in0=att_acc[j, h][:], scalar=1.0,
+                in1=residual_of[j][:, h * BANK : (h + 1) * BANK],
+                op0=ALU.mult, op1=ALU.add, accum_out=sums_of[j][:, h : h + 1],
+            )
+
+        def mean(j):
+            minus_mean_of[j] = stats.tile([P, 1], F32, name="minus_mean")
             nc.vector.tensor_scalar(
-                out=minus_mean[:], in0=sums[:, 0:1], scalar1=sums[:, 1:2], scalar2=-1.0 / SIZE,
+                out=minus_mean_of[j][:], in0=sums_of[j][:, 0:1], scalar1=sums_of[j][:, 1:2], scalar2=-1.0 / SIZE,
                 op0=ALU.add, op1=ALU.mult,
             )
-            squares = rows.tile([P, SIZE], BF16)
-            sum_squares = stats.tile([P, 1], F32)
-            nc.scalar.activation(
-                out=squares[:], in_=y[:], func=ACT.Square, bias=minus_mean[:], scale=1.0,
-                accum_out=sum_squares[:],
-            )
-            deviation = stats.tile([P, 1], F32)
-            nc.scalar.activation(out=deviation[:], in_=sum_squares[:], func=ACT.Sqrt, bias=eps[:], scale=1.0 / SIZE)
-            centred = rows.tile([P, SIZE], F32)
-            nc.vector.scalar_tensor_tensor(
-                out=centred[:], in0=y[:], scalar=minus_mean[:], in1=gain_all, op0=ALU.add, op1=ALU.mult,
-            )
-            return centred, deviation
 
-        def finish_rows(j, centred, deviation):
-            inverse = stats.tile([P, 1], F32)
-            nc.vector.reciprocal(out=inverse[:], in_=deviation[:])
-            result = rows.tile([P, SIZE], F32)
+        def sum_of_squares(j):
+            squares = rows.tile([P, SIZE], BF16)
+            sum_squares_of[j] = stats.tile([P, 1], F32, name="sum_squares")
+            nc.scalar.activation(
+                out=squares[:], in_=y_of[j][:], func=ACT.Square, bias=minus_mean_of[j][:], scale=1.0,
+                accum_out=sum_squares_of[j][:],
+            )
+
+        def deviation(j):
+            deviation_of[j] = stats.tile([P, 1], F32, name="deviation")
+            nc.scalar.activation(
+                out=deviation_of[j][:], in_=sum_squares_of[j][:], func=ACT.Sqrt, bias=eps[:], scale=1.0 / SIZE
+            )
+
+        def invert(j):
+            inverse_of[j] = stats.tile([P, 1], F32, name="inverse")
+            nc.vector.reciprocal(out=inverse_of[j][:], in_=deviation_of[j][:])
+
+        def centre(j):
+            centred_of[j] = rows.tile([P, SIZE], F32, name="centred")
             nc.vector.scalar_tensor_tensor(
-                out=result[:], in0=centred[:], scalar=inverse[:], in1=shift_all, op0=ALU.mult, op1=ALU.add,
+                out=centred_of[j][:], in0=y_of[j][:], scalar=minus_mean_of[j][:], in1=gain_all[:],
+                op0=ALU.add, op1=ALU.mult,
+            )
+
+        def finish(j):
+            result = rows.tile([P, SIZE], F32, bufs=3)
+            nc.vector.scalar_tensor_tensor(
+                out=result[:], in0=centred_of[j][:], scalar=inverse_of[j][:], in1=shift_all[:],
+                op0=ALU.mult, op1=ALU.add,
             )
             nc.sync.dma_start(out=out_rows[:, j, :], in_=result[:])
 
-        out_rows = out.rearrange("(p j) d -> p j d", j=TILES)
+        early = 2 * PAIRS
+        flip_pair(0)
+        for n in range(early):
+            flip_pair(n + 1)
+            quantise_pair(n)
 
-        quantise_matrix("wv", wv_sb)
-
-        spread = keep.tile([P, 3 * SIZE], BF16)
-        for v in range(3):
-            copies = psum_flip.tile([P, SIZE], BF16, tag="flip")
+        b_out_all = keep.tile([P, SIZE], BF16)
+        b_out_bank = psum_wide.tile([P, SIZE], BF16, tag="wide")
+        gain_all = psum_keep.tile([P, SIZE], BF16)
+        shift_all = psum_keep.tile([P, SIZE], BF16)
+        for v, bank in enumerate((b_out_bank, gain_all, shift_all)):
             for h in range(HALVES):
                 first = v * SIZE + h * BANK
                 nc.tensor.matmul(
-                    out=copies[:, h * BANK : (h + 1) * BANK], lhsT=ones[:], rhs=vectors[:, first : first + BANK],
+                    out=bank[:, h * BANK : (h + 1) * BANK], lhsT=ones[:], rhs=vectors[:, first : first + BANK],
                     start=True, stop=True,
                 )
-            nc.scalar.copy(out=spread[:, v * SIZE : (v + 1) * SIZE], in_=copies[:])
-        b_out_all = spread[:, 0:SIZE]
-        gain_all = spread[:, SIZE : 2 * SIZE]
-        shift_all = spread[:, 2 * SIZE : 3 * SIZE]
+        nc.scalar.copy(out=b_out_all[:], in_=b_out_bank[:])
 
-        quantise_matrix("feat", feat_sb)
-        residual = keep.tile([P, TILES * SIZE], F32)
-        for j in range(TILES):
-            nc.gpsimd.tensor_tensor(
-                out=residual[:, j * SIZE : (j + 1) * SIZE], in0=feat_sb[:, j * SIZE : (j + 1) * SIZE],
-                in1=b_out_all, op=ALU.add,
-            )
-        value_layer(0, 0)
-        value_layer(0, 1)
-        quantise_matrix("wo", wo_sb)
-
-        waiting = None
-        for j in range(TILES):
-            ahead = j + PASSES
-            if ahead < TILES:
-                value_layer(ahead // PASSES, ahead % PASSES)
-            centred, deviation = centre_rows(j)
-            if waiting is not None:
-                finish_rows(*waiting)
-            waiting = (j, centred, deviation)
-        finish_rows(*waiting)
+        units = range(PAIRS * PASSES)
+        tiles = range(TILES)
+        for s in range(early - len(pairs), TILES + 1):
+            n = s + len(pairs)
+            if n + 1 < len(pairs):
+                flip_pair(n + 1)
+            if n < len(pairs):
+                quantise_pair(n)
+            if s - 1 in tiles:
+                deviation(s - 1)
+            if s in tiles:
+                add_residual(s, 0)
+            if s - 1 in tiles:
+                invert(s - 1)
+            if s in tiles:
+                add_residual(s, 1)
+            if s + 2 in units:
+                value_quantise(s + 2)
+            if s + 1 in tiles:
+                output_matmuls(s + 1)
+            if s in tiles:
+                mean(s)
+            if s + 3 in units:
+                value_bias(s + 3, 0)
+            if s in tiles:
+                sum_of_squares(s)
+            if s - 1 in tiles:
+                finish(s - 1)
+            if s in tiles:
+                centre(s)
+            if s + 3 in units:
+                value_bias(s + 3, 1)
+            if s + 4 in units:
+                value_matmuls(s + 4)
+            if s + 2 in tiles:
+                add_b_out(s + 2)

@@ -55,17 +55,18 @@ def tile_efficientfusionlayer_pa_kernel(tc, feat, w_val, b_val, w_out, b_out, ga
         for name in ("wv", "feat", "wo"):
             raw[name] = keep.tile([P, TILES * SIZE], BF16, name="raw_" + name)
         wv_rows = w_val.rearrange("(r p e) d -> p r (e d)", p=P, e=2)
-        for r in range(PAIRS):
-            nc.sync.dma_start(out=raw["wv"][:, r * span : (r + 1) * span], in_=wv_rows[:, r, :])
         feat_rows = feat.rearrange("(p j) d -> p (j d)", j=TILES)
-        for r in range(PAIRS):
-            nc.sync.dma_start(out=raw["feat"][:, r * span : (r + 1) * span], in_=feat_rows[:, r * span : (r + 1) * span])
         wo_rows = w_out.rearrange("(i p) k -> p i k", p=P)
-        for r in range(PAIRS):
-            nc.sync.dma_start(
-                out=raw["wo"][:, r * span : (r + 1) * span].rearrange("p (i k) -> p i k", i=2),
-                in_=wo_rows[:, 2 * r : 2 * r + 2, :],
-            )
+        pairs = [("feat", 0)] + [("wv", r) for r in range(PAIRS)]
+        pairs += [("feat", r) for r in range(1, PAIRS)] + [("wo", r) for r in range(PAIRS)]
+        for name, r in pairs:
+            here = raw[name][:, r * span : (r + 1) * span]
+            if name == "wv":
+                nc.sync.dma_start(out=here, in_=wv_rows[:, r, :])
+            elif name == "feat":
+                nc.sync.dma_start(out=here, in_=feat_rows[:, r * span : (r + 1) * span])
+            else:
+                nc.sync.dma_start(out=here.rearrange("p (i k) -> p i k", i=2), in_=wo_rows[:, 2 * r : 2 * r + 2, :])
         out_rows = out.rearrange("(p j) d -> p j d", j=TILES)
 
         identity = keep.tile([P, P], F32)
@@ -75,7 +76,7 @@ def tile_efficientfusionlayer_pa_kernel(tc, feat, w_val, b_val, w_out, b_out, ga
         eps = keep.tile([P, 1], F32)
         nc.vector.memset(eps[:], EPS)
         warm = keep.tile([P, 1], F32)
-        nc.scalar.activation(out=warm[:], in_=eps[:], func=ACT.Sqrt)
+        nc.scalar.activation(out=warm[:], in_=eps[:], func=ACT.Abs_reciprocal_sqrt)
         bias_val = keep.tile([P, TILES], F32)
         nc.vector.tensor_copy(out=bias_val[:], in_=bias_bf[:])
 
@@ -85,7 +86,6 @@ def tile_efficientfusionlayer_pa_kernel(tc, feat, w_val, b_val, w_out, b_out, ga
             codes[name] = keep.tile([P, PASSES, SIZE], U32, name="codes_" + name, align_bytes=64)
             scales[name] = keep.tile([P, PASSES, SIZE], U8, name="scales_" + name, align_bytes=64)
 
-        pairs = [(name, r) for name in ("wv", "feat", "wo") for r in range(PAIRS)]
         grouped_of = {}
 
         def flip_pair(n):
@@ -115,50 +115,62 @@ def tile_efficientfusionlayer_pa_kernel(tc, feat, w_val, b_val, w_out, b_out, ga
                     in_=grouped_of[n][:, c * width : (c + 1) * width],
                 )
 
+        banks = range(PAIRS * PAIRS)
         val_acc = {}
         planes_of = {}
+        packed_of = {}
 
-        def value_matmuls(h):
-            cols = slice((h // PASSES) * PAIR, (h // PASSES + 1) * PAIR)
-            for half in range(2):
-                acc = psum_val.tile([P, 2, PAIR], F32)
-                for i in range(2):
-                    m = (h % PASSES) * PACK + 2 * half + i
-                    for c in range(PASSES):
-                        nc.tensor.matmul_mx(
-                            out=acc[:, i, :],
-                            lhsT=codes["wv"][:, c, m * P : (m + 1) * P].bitcast(FP8X4),
-                            lhsT_scale=scales["wv"][:, c, m * P : (m + 1) * P],
-                            rhs=codes["feat"][:, c, cols].bitcast(FP8X4),
-                            rhs_scale=scales["feat"][:, c, cols],
-                            start=(c == 0),
-                            stop=(c == PASSES - 1),
-                        )
-                val_acc[h, half] = acc
-
-        def value_bias(h, half):
-            if half == 0:
-                planes_of[h] = stage.tile([P, PACK, PAIR], BF16, name="planes")
+        def value_matmuls(q):
+            cols = slice((q // PAIRS) * PAIR, (q // PAIRS + 1) * PAIR)
+            acc = psum_val.tile([P, 2, PAIR], F32)
             for i in range(2):
-                t = 2 * half + i
-                m = (h % PASSES) * PACK + t
+                m = 2 * (q % PAIRS) + i
+                for c in range(PASSES):
+                    nc.tensor.matmul_mx(
+                        out=acc[:, i, :],
+                        lhsT=codes["wv"][:, c, m * P : (m + 1) * P].bitcast(FP8X4),
+                        lhsT_scale=scales["wv"][:, c, m * P : (m + 1) * P],
+                        rhs=codes["feat"][:, c, cols].bitcast(FP8X4),
+                        rhs_scale=scales["feat"][:, c, cols],
+                        start=(c == 0),
+                        stop=(c == PASSES - 1),
+                    )
+            val_acc[q] = acc
+
+        def value_bias(q):
+            if q % 2 == 0:
+                planes_of[q // 2] = stage.tile([P, PACK, PAIR], BF16, name="planes")
+            for i in range(2):
+                m = 2 * (q % PAIRS) + i
                 nc.scalar.activation(
-                    out=planes_of[h][:, t, :], in_=val_acc[h, half][:, i, :], func=ACT.Identity,
+                    out=planes_of[q // 2][:, m % PACK, :], in_=val_acc[q][:, i, :], func=ACT.Identity,
                     bias=bias_val[:, m : m + 1], scale=1.0,
                 )
 
-        def value_quantise(h):
-            cols = slice((h // PASSES) * PAIR, (h // PASSES + 1) * PAIR)
-            packed = stage.tile([P, PAIR * PACK], BF16, align_bytes=64)
-            nc.scalar.copy(
-                out=packed[:].rearrange("p (n i t) -> p n t i", i=4, t=PACK),
+        def value_pack(h):
+            packed_of[h] = stage.tile([P, PAIR * PACK], BF16, name="packed", align_bytes=64)
+            nc.vector.tensor_copy(
+                out=packed_of[h][:].rearrange("p (n i t) -> p n t i", i=4, t=PACK),
                 in_=planes_of[h][:].rearrange("p t (n i) -> p n t i", i=4),
             )
+
+        def value_quantise(h):
+            cols = slice((h // PASSES) * PAIR, (h // PASSES + 1) * PAIR)
             nc.vector.quantize_mx(
                 out=codes["val"][:, h % PASSES, cols].bitcast(FP8X4),
                 scales=scales["val"][:, h % PASSES, cols],
-                in_=packed[:],
+                in_=packed_of[h][:],
             )
+
+        def value_slot(i):
+            if i - 1 in banks:
+                value_matmuls(i - 1)
+            if i - 2 in banks:
+                value_bias(i - 2)
+            if i - 3 in banks and (i - 3) % 2 == 1:
+                value_pack((i - 3) // 2)
+            if i - 4 in banks and (i - 4) % 2 == 1:
+                value_quantise((i - 4) // 2)
 
         att_acc = {}
         residual_of = {}
@@ -166,7 +178,6 @@ def tile_efficientfusionlayer_pa_kernel(tc, feat, w_val, b_val, w_out, b_out, ga
         sums_of = {}
         minus_mean_of = {}
         sum_squares_of = {}
-        deviation_of = {}
         inverse_of = {}
         centred_of = {}
 
@@ -207,9 +218,10 @@ def tile_efficientfusionlayer_pa_kernel(tc, feat, w_val, b_val, w_out, b_out, ga
 
         def mean(j):
             minus_mean_of[j] = stats.tile([P, 1], F32, name="minus_mean")
-            nc.vector.tensor_scalar(
-                out=minus_mean_of[j][:], in0=sums_of[j][:, 0:1], scalar1=sums_of[j][:, 1:2], scalar2=-1.0 / SIZE,
-                op0=ALU.add, op1=ALU.mult,
+            shares = stats.tile([P, HALVES], F32)
+            nc.scalar.activation(
+                out=shares[:], in_=sums_of[j][:], func=ACT.Identity, scale=-1.0 / SIZE,
+                accum_out=minus_mean_of[j][:],
             )
 
         def sum_of_squares(j):
@@ -220,15 +232,12 @@ def tile_efficientfusionlayer_pa_kernel(tc, feat, w_val, b_val, w_out, b_out, ga
                 accum_out=sum_squares_of[j][:],
             )
 
-        def deviation(j):
-            deviation_of[j] = stats.tile([P, 1], F32, name="deviation")
-            nc.scalar.activation(
-                out=deviation_of[j][:], in_=sum_squares_of[j][:], func=ACT.Sqrt, bias=eps[:], scale=1.0 / SIZE
-            )
-
         def invert(j):
             inverse_of[j] = stats.tile([P, 1], F32, name="inverse")
-            nc.vector.reciprocal(out=inverse_of[j][:], in_=deviation_of[j][:])
+            nc.scalar.activation(
+                out=inverse_of[j][:], in_=sum_squares_of[j][:], func=ACT.Abs_reciprocal_sqrt, bias=eps[:],
+                scale=1.0 / SIZE,
+            )
 
         def centre(j):
             centred_of[j] = rows.tile([P, SIZE], F32, name="centred")
@@ -245,58 +254,50 @@ def tile_efficientfusionlayer_pa_kernel(tc, feat, w_val, b_val, w_out, b_out, ga
             )
             nc.sync.dma_start(out=out_rows[:, j, :], in_=result[:])
 
-        early = 2 * PAIRS
+        def spread_vectors():
+            for v, bank in enumerate((b_out_bank, gain_all, shift_all)):
+                for h in range(HALVES):
+                    first = v * SIZE + h * BANK
+                    nc.tensor.matmul(
+                        out=bank[:, h * BANK : (h + 1) * BANK], lhsT=ones[:], rhs=vectors[:, first : first + BANK],
+                        start=True, stop=True,
+                    )
+            nc.scalar.copy(out=b_out_all[:], in_=b_out_bank[:])
+
         flip_pair(0)
-        for n in range(early):
-            flip_pair(n + 1)
-            quantise_pair(n)
-
-        b_out_all = keep.tile([P, SIZE], BF16)
-        b_out_bank = psum_wide.tile([P, SIZE], BF16, tag="wide")
-        gain_all = psum_keep.tile([P, SIZE], BF16)
-        shift_all = psum_keep.tile([P, SIZE], BF16)
-        for v, bank in enumerate((b_out_bank, gain_all, shift_all)):
-            for h in range(HALVES):
-                first = v * SIZE + h * BANK
-                nc.tensor.matmul(
-                    out=bank[:, h * BANK : (h + 1) * BANK], lhsT=ones[:], rhs=vectors[:, first : first + BANK],
-                    start=True, stop=True,
-                )
-        nc.scalar.copy(out=b_out_all[:], in_=b_out_bank[:])
-
-        units = range(PAIRS * PASSES)
-        tiles = range(TILES)
-        for s in range(early - len(pairs), TILES + 1):
-            n = s + len(pairs)
+        for n in range(len(pairs)):
             if n + 1 < len(pairs):
                 flip_pair(n + 1)
-            if n < len(pairs):
-                quantise_pair(n)
-            if s - 1 in tiles:
-                deviation(s - 1)
-            if s in tiles:
-                add_residual(s, 0)
-            if s - 1 in tiles:
-                invert(s - 1)
-            if s in tiles:
-                add_residual(s, 1)
-            if s + 2 in units:
-                value_quantise(s + 2)
-            if s + 1 in tiles:
+            quantise_pair(n)
+            value_slot(n)
+            if pairs[n] == ("feat", PAIRS - 1):
+                b_out_all = keep.tile([P, SIZE], BF16)
+                b_out_bank = psum_wide.tile([P, SIZE], BF16, tag="wide")
+                gain_all = psum_keep.tile([P, SIZE], BF16)
+                shift_all = psum_keep.tile([P, SIZE], BF16)
+                spread_vectors()
+                add_b_out(0)
+                add_b_out(1)
+        output_matmuls(0)
+
+        for s in range(TILES + 1):
+            beat = len(pairs) + 2 * s
+            if s + 1 < TILES:
                 output_matmuls(s + 1)
-            if s in tiles:
+            if s > 0:
+                invert(s - 1)
+            if s < TILES:
+                add_residual(s, 0)
+            value_slot(beat)
+            if s < TILES:
+                add_residual(s, 1)
                 mean(s)
-            if s + 3 in units:
-                value_bias(s + 3, 0)
-            if s in tiles:
+            value_slot(beat + 1)
+            if s < TILES:
                 sum_of_squares(s)
-            if s - 1 in tiles:
+            if s > 0:
                 finish(s - 1)
-            if s in tiles:
+            if s < TILES:
                 centre(s)
-            if s + 3 in units:
-                value_bias(s + 3, 1)
-            if s + 4 in units:
-                value_matmuls(s + 4)
-            if s + 2 in tiles:
+            if s + 2 < TILES:
                 add_b_out(s + 2)

@@ -21,6 +21,7 @@ PAIRS = SIZE // PAIR
 BANK = 512
 HALVES = SIZE // BANK
 EPS = 1e-5
+EARLY_BEATS = 8
 
 FLOPS = 2 * 2 * SIZE * SIZE * SIZE
 
@@ -98,7 +99,7 @@ def tile_efficientfusionlayer_pa_kernel(tc, feat, w_val, b_val, w_out, b_out, ga
                 for block in range(2 * PASSES):
                     first = ((2 * r + i) * 2 * PASSES + block) * P
                     nc.tensor.transpose(flipped[:, block, :], words[:, first : first + P], identity[:])
-                copy_out = (nc.scalar.copy, nc.vector.tensor_copy)[i]
+                copy_out = nc.vector.tensor_copy if (name == "wo" and i == 1) else nc.scalar.copy
                 copy_out(
                     out=grouped_words[:, :, i * P : (i + 1) * P, :],
                     in_=flipped[:].rearrange("p (c u) r -> p c r u", u=2),
@@ -149,7 +150,7 @@ def tile_efficientfusionlayer_pa_kernel(tc, feat, w_val, b_val, w_out, b_out, ga
 
         def value_pack(h):
             packed_of[h] = stage.tile([P, PAIR * PACK], BF16, name="packed", align_bytes=64)
-            nc.vector.tensor_copy(
+            nc.scalar.copy(
                 out=packed_of[h][:].rearrange("p (n i t) -> p n t i", i=4, t=PACK),
                 in_=planes_of[h][:].rearrange("p t (n i) -> p n t i", i=4),
             )
@@ -247,43 +248,45 @@ def tile_efficientfusionlayer_pa_kernel(tc, feat, w_val, b_val, w_out, b_out, ga
             )
 
         def finish(j):
-            result = rows.tile([P, SIZE], F32, bufs=3)
-            nc.vector.scalar_tensor_tensor(
-                out=result[:], in0=centred_of[j][:], scalar=inverse_of[j][:], in1=shift_all[:],
-                op0=ALU.mult, op1=ALU.add,
-            )
-            nc.sync.dma_start(out=out_rows[:, j, :], in_=result[:])
+            for h in range(HALVES):
+                half = slice(h * BANK, (h + 1) * BANK)
+                result = rows.tile([P, BANK], F32, bufs=4)
+                nc.vector.scalar_tensor_tensor(
+                    out=result[:], in0=centred_of[j][:, half], scalar=inverse_of[j][:], in1=shift_all[:, half],
+                    op0=ALU.mult, op1=ALU.add,
+                )
+                nc.sync.dma_start(out=out_rows[:, j, half], in_=result[:])
 
-        def spread_vectors():
-            for v, bank in enumerate((b_out_bank, gain_all, shift_all)):
-                for h in range(HALVES):
-                    first = v * SIZE + h * BANK
-                    nc.tensor.matmul(
-                        out=bank[:, h * BANK : (h + 1) * BANK], lhsT=ones[:], rhs=vectors[:, first : first + BANK],
-                        start=True, stop=True,
-                    )
-            nc.scalar.copy(out=b_out_all[:], in_=b_out_bank[:])
+        def spread(v, bank):
+            for h in range(HALVES):
+                first = v * SIZE + h * BANK
+                nc.tensor.matmul(
+                    out=bank[:, h * BANK : (h + 1) * BANK], lhsT=ones[:], rhs=vectors[:, first : first + BANK],
+                    start=True, stop=True,
+                )
 
+        late = len(pairs) - EARLY_BEATS
         flip_pair(0)
         for n in range(len(pairs)):
             if n + 1 < len(pairs):
                 flip_pair(n + 1)
             quantise_pair(n)
-            value_slot(n)
+            value_slot(n - late)
             if pairs[n] == ("feat", PAIRS - 1):
                 b_out_all = keep.tile([P, SIZE], BF16)
                 b_out_bank = psum_wide.tile([P, SIZE], BF16, tag="wide")
-                gain_all = psum_keep.tile([P, SIZE], BF16)
-                shift_all = psum_keep.tile([P, SIZE], BF16)
-                spread_vectors()
+                spread(0, b_out_bank)
+                nc.scalar.copy(out=b_out_all[:], in_=b_out_bank[:])
                 add_b_out(0)
                 add_b_out(1)
         output_matmuls(0)
+        gain_all = psum_keep.tile([P, SIZE], BF16)
+        shift_all = psum_keep.tile([P, SIZE], BF16)
+        spread(1, gain_all)
+        spread(2, shift_all)
 
         for s in range(TILES + 1):
-            beat = len(pairs) + 2 * s
-            if s + 1 < TILES:
-                output_matmuls(s + 1)
+            beat = EARLY_BEATS + 2 * s
             if s > 0:
                 invert(s - 1)
             if s < TILES:
@@ -293,6 +296,8 @@ def tile_efficientfusionlayer_pa_kernel(tc, feat, w_val, b_val, w_out, b_out, ga
                 add_residual(s, 1)
                 mean(s)
             value_slot(beat + 1)
+            if s + 1 < TILES:
+                output_matmuls(s + 1)
             if s < TILES:
                 sum_of_squares(s)
             if s > 0:

@@ -21,7 +21,13 @@ PAIRS = SIZE // PAIR
 BANK = 512
 HALVES = SIZE // BANK
 EPS = 1e-5
-EARLY_BEATS = 8
+SCALAR_BANKS = ()
+VECTOR_FLIPS = 3
+VALUE_ROUNDS = (2, 3, 5, 6, 7, 8, 9, 10)
+RES_ROUNDS = (7, 8, 9, 10)
+RES_LEAD = 8
+RES_AT = 9
+GPSIMD_TILES = (0, 1, 2, 3, 4, 5)
 
 FLOPS = 2 * 2 * SIZE * SIZE * SIZE
 
@@ -30,16 +36,20 @@ def tile_efficientfusionlayer_pa_kernel(tc, feat, w_val, b_val, w_out, b_out, ga
     nc = tc.nc
     with ExitStack() as ctx:
         keep = ctx.enter_context(tc.tile_pool(name="keep", bufs=1))
-        stage = ctx.enter_context(tc.tile_pool(name="stage", bufs=3))
+        stage = ctx.enter_context(tc.tile_pool(name="stage", bufs=4))
         rows = ctx.enter_context(tc.tile_pool(name="rows", bufs=2))
         stats = ctx.enter_context(tc.tile_pool(name="stats", bufs=3))
         psum_keep = ctx.enter_context(tc.psum_pool(name="psum_keep", bufs=1))
         psum_wide = ctx.enter_context(tc.psum_pool(name="psum_wide", bufs=4))
-        psum_val = ctx.enter_context(tc.psum_pool(name="psum_val", bufs=2))
+        psum_val = ctx.enter_context(tc.psum_pool(name="psum_val", bufs=3))
         ctx.enter_context(tc.manual_schedule())
 
+        eps = keep.tile([P, 1], F32)
+        nc.vector.memset(eps[:], EPS)
+        warm = keep.tile([P, 1], F32)
+        nc.scalar.activation(out=warm[:], in_=eps[:], func=ACT.Abs_reciprocal_sqrt)
         vectors = keep.tile([P, 3 * SIZE], BF16)
-        nc.vector.memset(vectors[:], 0.0)
+        nc.vector.memset(vectors[:].bitcast(U32), 0)
         for v, vector in enumerate((b_out, gain, shift)):
             nc.scalar.dma_start(
                 out=vectors[0:1, v * SIZE : (v + 1) * SIZE], in_=vector.rearrange("(o d) -> o d", o=1)
@@ -58,34 +68,37 @@ def tile_efficientfusionlayer_pa_kernel(tc, feat, w_val, b_val, w_out, b_out, ga
         wv_rows = w_val.rearrange("(r p e) d -> p r (e d)", p=P, e=2)
         feat_rows = feat.rearrange("(p j) d -> p (j d)", j=TILES)
         wo_rows = w_out.rearrange("(i p) k -> p i k", p=P)
-        pairs = [("feat", 0)] + [("wv", r) for r in range(PAIRS)]
-        pairs += [("feat", r) for r in range(1, PAIRS)] + [("wo", r) for r in range(PAIRS)]
+        pairs = [("feat", 0), ("wv", 0), ("wv", 1), ("feat", 1), ("wv", 2), ("wv", 3), ("feat", 2), ("feat", 3)]
+        pairs += [("wo", r) for r in range(PAIRS)]
         for name, r in pairs:
             here = raw[name][:, r * span : (r + 1) * span]
             if name == "wv":
                 nc.sync.dma_start(out=here, in_=wv_rows[:, r, :])
             elif name == "feat":
-                nc.sync.dma_start(out=here, in_=feat_rows[:, r * span : (r + 1) * span])
+                pieces = 2 if r == 0 else 1
+                width = span // pieces
+                for first in range(r * span, (r + 1) * span, width):
+                    nc.sync.dma_start(
+                        out=raw[name][:, first : first + width], in_=feat_rows[:, first : first + width]
+                    )
             else:
                 nc.sync.dma_start(out=here.rearrange("p (i k) -> p i k", i=2), in_=wo_rows[:, 2 * r : 2 * r + 2, :])
         out_rows = out.rearrange("(p j) d -> p j d", j=TILES)
 
         identity = keep.tile([P, P], F32)
         make_identity(nc, identity[:])
+        identity_bf = keep.tile([P, P], BF16)
+        make_identity(nc, identity_bf[:])
         ones = keep.tile([P, P], BF16)
         nc.vector.memset(ones[:], 1.0)
-        eps = keep.tile([P, 1], F32)
-        nc.vector.memset(eps[:], EPS)
-        warm = keep.tile([P, 1], F32)
-        nc.scalar.activation(out=warm[:], in_=eps[:], func=ACT.Abs_reciprocal_sqrt)
         bias_val = keep.tile([P, TILES], F32)
-        nc.vector.tensor_copy(out=bias_val[:], in_=bias_bf[:])
+        nc.scalar.copy(out=bias_val[:], in_=bias_bf[:])
 
         codes = {}
         scales = {}
         for name in ("wv", "feat", "wo", "val"):
-            codes[name] = keep.tile([P, PASSES, SIZE], U32, name="codes_" + name, align_bytes=64)
-            scales[name] = keep.tile([P, PASSES, SIZE], U8, name="scales_" + name, align_bytes=64)
+            codes[name] = keep.tile([P, PAIRS, PASSES, PAIR], U32, name="codes_" + name, align_bytes=64)
+            scales[name] = keep.tile([P, PAIRS, PASSES, PAIR], U8, name="scales_" + name, align_bytes=64)
 
         grouped_of = {}
 
@@ -99,7 +112,7 @@ def tile_efficientfusionlayer_pa_kernel(tc, feat, w_val, b_val, w_out, b_out, ga
                 for block in range(2 * PASSES):
                     first = ((2 * r + i) * 2 * PASSES + block) * P
                     nc.tensor.transpose(flipped[:, block, :], words[:, first : first + P], identity[:])
-                copy_out = nc.vector.tensor_copy if (name == "wo" and i == 1) else nc.scalar.copy
+                copy_out = nc.vector.tensor_copy if (n < VECTOR_FLIPS and i == 1) else nc.scalar.copy
                 copy_out(
                     out=grouped_words[:, :, i * P : (i + 1) * P, :],
                     in_=flipped[:].rearrange("p (c u) r -> p c r u", u=2),
@@ -108,70 +121,78 @@ def tile_efficientfusionlayer_pa_kernel(tc, feat, w_val, b_val, w_out, b_out, ga
 
         def quantise_pair(n):
             name, r = pairs[n]
-            width = PAIR * PACK
-            for c in range(PASSES):
-                nc.vector.quantize_mx(
-                    out=codes[name][:, c, r * PAIR : (r + 1) * PAIR].bitcast(FP8X4),
-                    scales=scales[name][:, c, r * PAIR : (r + 1) * PAIR],
-                    in_=grouped_of[n][:, c * width : (c + 1) * width],
-                )
+            nc.vector.quantize_mx(
+                out=codes[name][:, r].rearrange("p c n -> p (c n)").bitcast(FP8X4),
+                scales=scales[name][:, r].rearrange("p c n -> p (c n)"),
+                in_=grouped_of[n][:],
+            )
 
-        banks = range(PAIRS * PAIRS)
+        blocks = [(0, 0), (1, 0), (0, 1), (1, 1), (2, 0), (2, 1), (3, 0), (3, 1)]
         val_acc = {}
         planes_of = {}
+        scalar_banks = SCALAR_BANKS
         packed_of = {}
 
+        def tile_of(name, j, c):
+            cols = slice((j % 2) * P, (j % 2 + 1) * P)
+            return codes[name][:, j // 2, c, cols].bitcast(FP8X4), scales[name][:, j // 2, c, cols]
+
         def value_matmuls(q):
-            cols = slice((q // PAIRS) * PAIR, (q // PAIRS + 1) * PAIR)
-            acc = psum_val.tile([P, 2, PAIR], F32)
-            for i in range(2):
-                m = 2 * (q % PAIRS) + i
+            r, c_val = blocks[q // 2]
+            acc = psum_val.tile([P, PACK, P], F32, name="acc")
+            for t in range(PACK):
                 for c in range(PASSES):
+                    lhsT, lhsT_scale = tile_of("wv", PACK * c_val + t, c)
+                    rhs, rhs_scale = tile_of("feat", 2 * r + q % 2, c)
                     nc.tensor.matmul_mx(
-                        out=acc[:, i, :],
-                        lhsT=codes["wv"][:, c, m * P : (m + 1) * P].bitcast(FP8X4),
-                        lhsT_scale=scales["wv"][:, c, m * P : (m + 1) * P],
-                        rhs=codes["feat"][:, c, cols].bitcast(FP8X4),
-                        rhs_scale=scales["feat"][:, c, cols],
-                        start=(c == 0),
-                        stop=(c == PASSES - 1),
+                        out=acc[:, t, :], lhsT=lhsT, lhsT_scale=lhsT_scale, rhs=rhs, rhs_scale=rhs_scale,
+                        start=(c == 0), stop=(c == PASSES - 1),
                     )
             val_acc[q] = acc
 
         def value_bias(q):
             if q % 2 == 0:
-                planes_of[q // 2] = stage.tile([P, PACK, PAIR], BF16, name="planes")
-            for i in range(2):
-                m = 2 * (q % PAIRS) + i
+                packed_of[q // 2] = stage.tile([P, PAIR * PACK], BF16, name="packed", align_bytes=64)
+            first = (q % 2) * P * PACK
+            c_val = blocks[q // 2][1]
+            nc.vector.tensor_tensor(
+                out=packed_of[q // 2][:, first : first + P * PACK].rearrange("p (n t) -> p n t", t=PACK),
+                in0=val_acc[q][:].rearrange("p t n -> p n t"),
+                in1=bias_bf[:, c_val * PACK : (c_val + 1) * PACK].unsqueeze(1).to_broadcast([P, P, PACK]),
+                op=ALU.add,
+            )
+
+        def value_bias_on_scalar(q):
+            c_val = blocks[q // 2][1]
+            planes_of[q] = stage.tile([P, PACK, P], BF16, name="planes")
+            for t in range(PACK):
+                m = c_val * PACK + t
                 nc.scalar.activation(
-                    out=planes_of[q // 2][:, m % PACK, :], in_=val_acc[q][:, i, :], func=ACT.Identity,
+                    out=planes_of[q][:, t, :], in_=val_acc[q][:, t, :], func=ACT.Identity,
                     bias=bias_val[:, m : m + 1], scale=1.0,
                 )
 
-        def value_pack(h):
-            packed_of[h] = stage.tile([P, PAIR * PACK], BF16, name="packed", align_bytes=64)
+        def value_pack(q):
+            if q % 2 == 0:
+                packed_of[q // 2] = stage.tile([P, PAIR * PACK], BF16, name="packed", align_bytes=64)
+            first = (q % 2) * P * PACK
             nc.scalar.copy(
-                out=packed_of[h][:].rearrange("p (n i t) -> p n t i", i=4, t=PACK),
-                in_=planes_of[h][:].rearrange("p t (n i) -> p n t i", i=4),
+                out=packed_of[q // 2][:, first : first + P * PACK].rearrange("p (n i t) -> p n t i", i=4, t=PACK),
+                in_=planes_of[q][:].rearrange("p t (n i) -> p n t i", i=4),
             )
 
         def value_quantise(h):
-            cols = slice((h // PASSES) * PAIR, (h // PASSES + 1) * PAIR)
+            r, c_val = blocks[h]
             nc.vector.quantize_mx(
-                out=codes["val"][:, h % PASSES, cols].bitcast(FP8X4),
-                scales=scales["val"][:, h % PASSES, cols],
-                in_=packed_of[h][:],
+                out=codes["val"][:, r, c_val].bitcast(FP8X4), scales=scales["val"][:, r, c_val], in_=packed_of[h][:],
             )
 
-        def value_slot(i):
-            if i - 1 in banks:
-                value_matmuls(i - 1)
-            if i - 2 in banks:
-                value_bias(i - 2)
-            if i - 3 in banks and (i - 3) % 2 == 1:
-                value_pack((i - 3) // 2)
-            if i - 4 in banks and (i - 4) % 2 == 1:
-                value_quantise((i - 4) // 2)
+        def value_empty(q):
+            if q in scalar_banks:
+                value_bias_on_scalar(q)
+                value_pack(q)
+            else:
+                value_bias(q)
 
         att_acc = {}
         residual_of = {}
@@ -183,7 +204,7 @@ def tile_efficientfusionlayer_pa_kernel(tc, feat, w_val, b_val, w_out, b_out, ga
         centred_of = {}
 
         def add_b_out(j):
-            residual_of[j] = rows.tile([P, SIZE], F32, name="residual")
+            residual_of[j] = rows.tile([P, SIZE], F32, name="residual", bufs=8)
             for h in range(HALVES):
                 nc.gpsimd.tensor_tensor(
                     out=residual_of[j][:, h * BANK : (h + 1) * BANK],
@@ -191,25 +212,35 @@ def tile_efficientfusionlayer_pa_kernel(tc, feat, w_val, b_val, w_out, b_out, ga
                     in1=b_out_all[:, h * BANK : (h + 1) * BANK], op=ALU.add,
                 )
 
+        def residual_half(j, h):
+            if h == 0:
+                residual_of[j] = rows.tile([P, SIZE], F32, name="residual", bufs=8)
+            bank = psum_wide.tile([P, BANK], F32, tag="wide")
+            half = slice(h * BANK, (h + 1) * BANK)
+            nc.tensor.matmul(
+                out=bank[:], lhsT=identity_bf[:], rhs=raw["feat"][:, j * SIZE + h * BANK : j * SIZE + (h + 1) * BANK],
+                start=True, stop=False,
+            )
+            nc.tensor.matmul(out=bank[:], lhsT=ones[:], rhs=vectors[:, half], start=False, stop=True)
+            nc.scalar.copy(out=residual_of[j][:, half], in_=bank[:])
+
         def output_matmuls(j):
-            cols = slice(j * P, (j + 1) * P)
             for h in range(HALVES):
                 acc = psum_wide.tile([P, BANK], F32, tag="wide")
-                for c in range(PASSES):
-                    nc.tensor.matmul_mx(
-                        out=acc[:],
-                        lhsT=codes["val"][:, c, cols].bitcast(FP8X4),
-                        lhsT_scale=scales["val"][:, c, cols],
-                        rhs=codes["wo"][:, c, h * BANK : (h + 1) * BANK].bitcast(FP8X4),
-                        rhs_scale=scales["wo"][:, c, h * BANK : (h + 1) * BANK],
-                        start=(c == 0),
-                        stop=(c == PASSES - 1),
-                    )
+                for i in range(2):
+                    r = 2 * h + i
+                    for c in range(PASSES):
+                        lhsT, lhsT_scale = tile_of("val", j, c)
+                        nc.tensor.matmul_mx(
+                            out=acc[:, i * PAIR : (i + 1) * PAIR], lhsT=lhsT, lhsT_scale=lhsT_scale,
+                            rhs=codes["wo"][:, r, c].bitcast(FP8X4), rhs_scale=scales["wo"][:, r, c],
+                            start=(c == 0), stop=(c == PASSES - 1),
+                        )
                 att_acc[j, h] = acc
 
         def add_residual(j, h):
             if h == 0:
-                y_of[j] = rows.tile([P, SIZE], F32, name="y")
+                y_of[j] = rows.tile([P, SIZE], F32, name="y", bufs=3)
                 sums_of[j] = stats.tile([P, HALVES], F32, name="sums")
             nc.vector.scalar_tensor_tensor(
                 out=y_of[j][:, h * BANK : (h + 1) * BANK], in0=att_acc[j, h][:], scalar=1.0,
@@ -241,11 +272,22 @@ def tile_efficientfusionlayer_pa_kernel(tc, feat, w_val, b_val, w_out, b_out, ga
             )
 
         def centre(j):
-            centred_of[j] = rows.tile([P, SIZE], F32, name="centred")
+            centred_of[j] = rows.tile([P, SIZE], F32, name="centred", bufs=3)
             nc.vector.scalar_tensor_tensor(
                 out=centred_of[j][:], in0=y_of[j][:], scalar=minus_mean_of[j][:], in1=gain_all[:],
                 op0=ALU.add, op1=ALU.mult,
             )
+
+        def scale_rows(j):
+            scaled = rows.tile([P, SIZE], F32, bufs=3)
+            nc.scalar.activation(
+                out=scaled[:], in_=centred_of[j][:], func=ACT.Copy, scale=inverse_of[j][:],
+            )
+            for h in range(HALVES):
+                half = slice(h * BANK, (h + 1) * BANK)
+                result = rows.tile([P, BANK], F32, bufs=4)
+                nc.gpsimd.tensor_tensor(out=result[:], in0=scaled[:, half], in1=shift_all_sb[:, half], op=ALU.add)
+                nc.sync.dma_start(out=out_rows[:, j, half], in_=result[:])
 
         def finish(j):
             for h in range(HALVES):
@@ -265,44 +307,68 @@ def tile_efficientfusionlayer_pa_kernel(tc, feat, w_val, b_val, w_out, b_out, ga
                     start=True, stop=True,
                 )
 
-        late = len(pairs) - EARLY_BEATS
+        value_rounds = VALUE_ROUNDS
         flip_pair(0)
-        for n in range(len(pairs)):
+        flip_pair(1)
+        quantise_pair(0)
+        previous = None
+        h = 0
+        for n in range(len(pairs) + 1):
+            if n == RES_AT:
+                for j in range(len(RES_ROUNDS) // 2, RES_LEAD):
+                    add_b_out(j)
             if n + 1 < len(pairs):
-                flip_pair(n + 1)
-            quantise_pair(n)
-            value_slot(n - late)
-            if pairs[n] == ("feat", PAIRS - 1):
+                quantise_pair(n + 1)
+            if previous is not None:
+                value_empty(2 * previous + 1)
+            current = None
+            if n in value_rounds:
+                current = h
+                h += 1
+                value_matmuls(2 * current)
+                value_matmuls(2 * current + 1)
+            if n + 2 < len(pairs):
+                flip_pair(n + 2)
+            if current is not None:
+                value_empty(2 * current)
+            if previous is not None:
+                value_quantise(previous)
+            previous = current
+            if n in RES_ROUNDS:
+                half = RES_ROUNDS.index(n)
+                residual_half(half // 2, half % 2)
+            if n == 4:
                 b_out_all = keep.tile([P, SIZE], BF16)
-                b_out_bank = psum_wide.tile([P, SIZE], BF16, tag="wide")
+                b_out_bank = psum_keep.tile([P, SIZE], BF16, name="gain_all")
                 spread(0, b_out_bank)
                 nc.scalar.copy(out=b_out_all[:], in_=b_out_bank[:])
-                add_b_out(0)
-                add_b_out(1)
+            if n == 9:
+                gain_all = psum_keep.tile([P, SIZE], BF16, name="gain_all")
+                spread(1, gain_all)
         output_matmuls(0)
-        gain_all = psum_keep.tile([P, SIZE], BF16)
-        shift_all = psum_keep.tile([P, SIZE], BF16)
-        spread(1, gain_all)
+        shift_all = psum_val.tile([P, SIZE], BF16, name="acc")
         spread(2, shift_all)
+        shift_all_sb = keep.tile([P, SIZE], BF16)
+        nc.scalar.copy(out=shift_all_sb[:], in_=shift_all[:])
 
-        for s in range(TILES + 1):
-            beat = EARLY_BEATS + 2 * s
-            if s > 0:
-                invert(s - 1)
-            if s < TILES:
-                add_residual(s, 0)
-            value_slot(beat)
-            if s < TILES:
-                add_residual(s, 1)
-                mean(s)
-            value_slot(beat + 1)
+        gpsimd_tiles = GPSIMD_TILES
+        for s in range(TILES + 2):
             if s + 1 < TILES:
                 output_matmuls(s + 1)
             if s < TILES:
-                sum_of_squares(s)
-            if s > 0:
-                finish(s - 1)
+                add_residual(s, 0)
+            if 0 <= s - 1 < TILES:
+                mean(s - 1)
+                centre(s - 1)
+                if (s - 2) in gpsimd_tiles:
+                    scale_rows(s - 2)
+                sum_of_squares(s - 1)
+                invert(s - 1)
+            elif (s - 2) in gpsimd_tiles:
+                scale_rows(s - 2)
+            if 0 <= s - 2 and not (s - 2) in gpsimd_tiles:
+                finish(s - 2)
             if s < TILES:
-                centre(s)
-            if s + 2 < TILES:
-                add_b_out(s + 2)
+                add_residual(s, 1)
+            if s + RES_LEAD < TILES:
+                add_b_out(s + RES_LEAD)

@@ -21,13 +21,19 @@ PAIRS = SIZE // PAIR
 BANK = 512
 HALVES = SIZE // BANK
 EPS = 1e-5
-SCALAR_BANKS = ()
-VECTOR_FLIPS = 3
+FLIP_LEAD = 2
+FLIP_FIRST = True
+STAGE = 5
+SCALAR_BANKS = (5, 9, 13)
+VECTOR_FLIPS = 2
 VALUE_ROUNDS = (2, 3, 5, 6, 7, 8, 9, 10)
-RES_ROUNDS = (7, 8, 9, 10)
-RES_LEAD = 8
-RES_AT = 9
-GPSIMD_TILES = (0, 1, 2, 3, 4, 5)
+VALUE_STEPS = ()
+ORDER_TAIL = [("feat", 2), ("feat", 3)] + [("wo", r) for r in range(4)]
+RES_BUFS = 2
+RES_ROUNDS = ()
+RES_LEAD = 2
+B_OUT_AT = 1
+GPSIMD_TILES = (1, 3, 5)
 
 FLOPS = 2 * 2 * SIZE * SIZE * SIZE
 
@@ -36,7 +42,7 @@ def tile_efficientfusionlayer_pa_kernel(tc, feat, w_val, b_val, w_out, b_out, ga
     nc = tc.nc
     with ExitStack() as ctx:
         keep = ctx.enter_context(tc.tile_pool(name="keep", bufs=1))
-        stage = ctx.enter_context(tc.tile_pool(name="stage", bufs=4))
+        stage = ctx.enter_context(tc.tile_pool(name="stage", bufs=STAGE))
         rows = ctx.enter_context(tc.tile_pool(name="rows", bufs=2))
         stats = ctx.enter_context(tc.tile_pool(name="stats", bufs=3))
         psum_keep = ctx.enter_context(tc.psum_pool(name="psum_keep", bufs=1))
@@ -46,20 +52,21 @@ def tile_efficientfusionlayer_pa_kernel(tc, feat, w_val, b_val, w_out, b_out, ga
 
         eps = keep.tile([P, 1], F32)
         nc.vector.memset(eps[:], EPS)
-        warm = keep.tile([P, 1], F32)
-        nc.scalar.activation(out=warm[:], in_=eps[:], func=ACT.Abs_reciprocal_sqrt)
-        vectors = keep.tile([P, 3 * SIZE], BF16)
-        nc.vector.memset(vectors[:].bitcast(U32), 0)
-        for v, vector in enumerate((b_out, gain, shift)):
-            nc.scalar.dma_start(
-                out=vectors[0:1, v * SIZE : (v + 1) * SIZE], in_=vector.rearrange("(o d) -> o d", o=1)
-            )
         bias_bf = keep.tile([P, TILES], BF16)
         with nc.allow_non_contiguous_dma(reason="1024 bias values, two to a piece"):
             nc.scalar.dma_start(
                 out=bias_bf[:].rearrange("p (r e) -> p r e", e=2),
                 in_=b_val.rearrange("(r p e) -> p r e", p=P, e=2),
             )
+        vectors = keep.tile([P, 3 * SIZE], BF16)
+        nc.vector.memset(vectors[:].bitcast(U32), 0)
+        for v, vector in enumerate((b_out, gain, shift)):
+            nc.scalar.dma_start(
+                out=vectors[0:1, v * SIZE : (v + 1) * SIZE], in_=vector.rearrange("(o d) -> o d", o=1)
+            )
+
+        warm = keep.tile([P, 1], F32)
+        nc.scalar.activation(out=warm[:], in_=eps[:], func=ACT.Abs_reciprocal_sqrt)
 
         span = 2 * SIZE
         raw = {}
@@ -68,8 +75,8 @@ def tile_efficientfusionlayer_pa_kernel(tc, feat, w_val, b_val, w_out, b_out, ga
         wv_rows = w_val.rearrange("(r p e) d -> p r (e d)", p=P, e=2)
         feat_rows = feat.rearrange("(p j) d -> p (j d)", j=TILES)
         wo_rows = w_out.rearrange("(i p) k -> p i k", p=P)
-        pairs = [("feat", 0), ("wv", 0), ("wv", 1), ("feat", 1), ("wv", 2), ("wv", 3), ("feat", 2), ("feat", 3)]
-        pairs += [("wo", r) for r in range(PAIRS)]
+        pairs = [("feat", 0), ("wv", 0), ("wv", 1), ("feat", 1), ("wv", 2), ("wv", 3)]
+        pairs += ORDER_TAIL
         for name, r in pairs:
             here = raw[name][:, r * span : (r + 1) * span]
             if name == "wv":
@@ -91,8 +98,8 @@ def tile_efficientfusionlayer_pa_kernel(tc, feat, w_val, b_val, w_out, b_out, ga
         make_identity(nc, identity_bf[:])
         ones = keep.tile([P, P], BF16)
         nc.vector.memset(ones[:], 1.0)
+        scalar_banks = SCALAR_BANKS
         bias_val = keep.tile([P, TILES], F32)
-        nc.scalar.copy(out=bias_val[:], in_=bias_bf[:])
 
         codes = {}
         scales = {}
@@ -130,7 +137,6 @@ def tile_efficientfusionlayer_pa_kernel(tc, feat, w_val, b_val, w_out, b_out, ga
         blocks = [(0, 0), (1, 0), (0, 1), (1, 1), (2, 0), (2, 1), (3, 0), (3, 1)]
         val_acc = {}
         planes_of = {}
-        scalar_banks = SCALAR_BANKS
         packed_of = {}
 
         def tile_of(name, j, c):
@@ -204,7 +210,7 @@ def tile_efficientfusionlayer_pa_kernel(tc, feat, w_val, b_val, w_out, b_out, ga
         centred_of = {}
 
         def add_b_out(j):
-            residual_of[j] = rows.tile([P, SIZE], F32, name="residual", bufs=8)
+            residual_of[j] = rows.tile([P, SIZE], F32, name="residual", bufs=RES_BUFS)
             for h in range(HALVES):
                 nc.gpsimd.tensor_tensor(
                     out=residual_of[j][:, h * BANK : (h + 1) * BANK],
@@ -214,7 +220,7 @@ def tile_efficientfusionlayer_pa_kernel(tc, feat, w_val, b_val, w_out, b_out, ga
 
         def residual_half(j, h):
             if h == 0:
-                residual_of[j] = rows.tile([P, SIZE], F32, name="residual", bufs=8)
+                residual_of[j] = rows.tile([P, SIZE], F32, name="residual", bufs=RES_BUFS)
             bank = psum_wide.tile([P, BANK], F32, tag="wide")
             half = slice(h * BANK, (h + 1) * BANK)
             nc.tensor.matmul(
@@ -308,27 +314,26 @@ def tile_efficientfusionlayer_pa_kernel(tc, feat, w_val, b_val, w_out, b_out, ga
                 )
 
         value_rounds = VALUE_ROUNDS
-        flip_pair(0)
-        flip_pair(1)
+        for n in range(FLIP_LEAD):
+            flip_pair(n)
         quantise_pair(0)
         previous = None
         h = 0
         for n in range(len(pairs) + 1):
-            if n == RES_AT:
-                for j in range(len(RES_ROUNDS) // 2, RES_LEAD):
-                    add_b_out(j)
             if n + 1 < len(pairs):
                 quantise_pair(n + 1)
             if previous is not None:
                 value_empty(2 * previous + 1)
+            if FLIP_FIRST and n + FLIP_LEAD < len(pairs):
+                flip_pair(n + FLIP_LEAD)
             current = None
             if n in value_rounds:
                 current = h
                 h += 1
                 value_matmuls(2 * current)
                 value_matmuls(2 * current + 1)
-            if n + 2 < len(pairs):
-                flip_pair(n + 2)
+            if not FLIP_FIRST and n + FLIP_LEAD < len(pairs):
+                flip_pair(n + FLIP_LEAD)
             if current is not None:
                 value_empty(2 * current)
             if previous is not None:
@@ -337,38 +342,56 @@ def tile_efficientfusionlayer_pa_kernel(tc, feat, w_val, b_val, w_out, b_out, ga
             if n in RES_ROUNDS:
                 half = RES_ROUNDS.index(n)
                 residual_half(half // 2, half % 2)
-            if n == 4:
+            if n == B_OUT_AT:
                 b_out_all = keep.tile([P, SIZE], BF16)
                 b_out_bank = psum_keep.tile([P, SIZE], BF16, name="gain_all")
                 spread(0, b_out_bank)
                 nc.scalar.copy(out=b_out_all[:], in_=b_out_bank[:])
+                if scalar_banks:
+                    nc.scalar.copy(out=bias_val[:], in_=bias_bf[:])
+                for j in range(RES_LEAD):
+                    add_b_out(j)
             if n == 9:
-                gain_all = psum_keep.tile([P, SIZE], BF16, name="gain_all")
-                spread(1, gain_all)
+                pass
         output_matmuls(0)
+        gain_all = psum_keep.tile([P, SIZE], BF16, name="gain_all")
+        spread(1, gain_all)
         shift_all = psum_val.tile([P, SIZE], BF16, name="acc")
         spread(2, shift_all)
         shift_all_sb = keep.tile([P, SIZE], BF16)
         nc.scalar.copy(out=shift_all_sb[:], in_=shift_all[:])
 
         gpsimd_tiles = GPSIMD_TILES
+        value_steps = VALUE_STEPS
         for s in range(TILES + 2):
             if s + 1 < TILES:
                 output_matmuls(s + 1)
+            current = None
+            if s in value_steps:
+                current = h
+                h += 1
+                value_matmuls(2 * current)
+                value_matmuls(2 * current + 1)
             if s < TILES:
                 add_residual(s, 0)
             if 0 <= s - 1 < TILES:
                 mean(s - 1)
                 centre(s - 1)
-                if (s - 2) in gpsimd_tiles:
-                    scale_rows(s - 2)
+            if (s - 2) in gpsimd_tiles:
+                scale_rows(s - 2)
+            if 0 <= s - 1 < TILES:
                 sum_of_squares(s - 1)
                 invert(s - 1)
-            elif (s - 2) in gpsimd_tiles:
-                scale_rows(s - 2)
             if 0 <= s - 2 and not (s - 2) in gpsimd_tiles:
                 finish(s - 2)
+            if current is not None:
+                value_empty(2 * current)
             if s < TILES:
                 add_residual(s, 1)
+            if current is not None:
+                value_empty(2 * current + 1)
+            if previous is not None:
+                value_quantise(previous)
+            previous = current
             if s + RES_LEAD < TILES:
                 add_b_out(s + RES_LEAD)

@@ -21,19 +21,24 @@ PAIRS = SIZE // PAIR
 BANK = 512
 HALVES = SIZE // BANK
 EPS = 1e-5
+LATE_AT = 11
+SHIFT_AT = 10
+SHIFT_PSUM = True
+SCALE_LATE = False
 FLIP_LEAD = 2
 FLIP_FIRST = True
 STAGE = 5
 SCALAR_BANKS = (5, 9, 13)
-VECTOR_FLIPS = 2
-VALUE_ROUNDS = (2, 3, 5, 6, 7, 8, 9, 10)
-VALUE_STEPS = ()
+VECTOR_FLIPS = 3
+ROUND_BANKS = {2: (0, 1), 3: (2, 3), 5: (4, 5), 6: (6, 7), 7: (8, 9), 8: (10, 11), 9: (12, 13), 10: (14, 15)}
+STEP_BANKS = {}
 ORDER_TAIL = [("feat", 2), ("feat", 3)] + [("wo", r) for r in range(4)]
-RES_BUFS = 2
-RES_ROUNDS = ()
-RES_LEAD = 2
+RES_BUFS = 3
+RES_ROUNDS = {}
+PE_TILES = ()
+RES_FIRST = 2
 B_OUT_AT = 1
-GPSIMD_TILES = (1, 3, 5)
+GPSIMD_TILES = (0, 2, 3, 5)
 
 FLOPS = 2 * 2 * SIZE * SIZE * SIZE
 
@@ -47,7 +52,7 @@ def tile_efficientfusionlayer_pa_kernel(tc, feat, w_val, b_val, w_out, b_out, ga
         stats = ctx.enter_context(tc.tile_pool(name="stats", bufs=3))
         psum_keep = ctx.enter_context(tc.psum_pool(name="psum_keep", bufs=1))
         psum_wide = ctx.enter_context(tc.psum_pool(name="psum_wide", bufs=4))
-        psum_val = ctx.enter_context(tc.psum_pool(name="psum_val", bufs=3))
+        psum_val = ctx.enter_context(tc.psum_pool(name="psum_val", bufs=2))
         ctx.enter_context(tc.manual_schedule())
 
         eps = keep.tile([P, 1], F32)
@@ -58,6 +63,8 @@ def tile_efficientfusionlayer_pa_kernel(tc, feat, w_val, b_val, w_out, b_out, ga
                 out=bias_bf[:].rearrange("p (r e) -> p r e", e=2),
                 in_=b_val.rearrange("(r p e) -> p r e", p=P, e=2),
             )
+        warm = keep.tile([P, 1], F32)
+        nc.scalar.activation(out=warm[:], in_=eps[:], func=ACT.Abs_reciprocal_sqrt)
         vectors = keep.tile([P, 3 * SIZE], BF16)
         nc.vector.memset(vectors[:].bitcast(U32), 0)
         for v, vector in enumerate((b_out, gain, shift)):
@@ -65,8 +72,6 @@ def tile_efficientfusionlayer_pa_kernel(tc, feat, w_val, b_val, w_out, b_out, ga
                 out=vectors[0:1, v * SIZE : (v + 1) * SIZE], in_=vector.rearrange("(o d) -> o d", o=1)
             )
 
-        warm = keep.tile([P, 1], F32)
-        nc.scalar.activation(out=warm[:], in_=eps[:], func=ACT.Abs_reciprocal_sqrt)
 
         span = 2 * SIZE
         raw = {}
@@ -136,6 +141,7 @@ def tile_efficientfusionlayer_pa_kernel(tc, feat, w_val, b_val, w_out, b_out, ga
 
         blocks = [(0, 0), (1, 0), (0, 1), (1, 1), (2, 0), (2, 1), (3, 0), (3, 1)]
         val_acc = {}
+        shift_placed = []
         planes_of = {}
         packed_of = {}
 
@@ -145,7 +151,8 @@ def tile_efficientfusionlayer_pa_kernel(tc, feat, w_val, b_val, w_out, b_out, ga
 
         def value_matmuls(q):
             r, c_val = blocks[q // 2]
-            acc = psum_val.tile([P, PACK, P], F32, name="acc")
+            spare = q % 3 == 2 and not shift_placed
+            acc = psum_val.tile([P, PACK, P], F32, tag="spare" if spare else "acc", bufs=1 if spare else 2)
             for t in range(PACK):
                 for c in range(PASSES):
                     lhsT, lhsT_scale = tile_of("wv", PACK * c_val + t, c)
@@ -215,7 +222,7 @@ def tile_efficientfusionlayer_pa_kernel(tc, feat, w_val, b_val, w_out, b_out, ga
                 nc.gpsimd.tensor_tensor(
                     out=residual_of[j][:, h * BANK : (h + 1) * BANK],
                     in0=raw["feat"][:, j * SIZE + h * BANK : j * SIZE + (h + 1) * BANK],
-                    in1=b_out_all[:, h * BANK : (h + 1) * BANK], op=ALU.add,
+                    in1=(b_out_all if j < RES_FIRST else b_out_late)[:, h * BANK : (h + 1) * BANK], op=ALU.add,
                 )
 
         def residual_half(j, h):
@@ -296,9 +303,11 @@ def tile_efficientfusionlayer_pa_kernel(tc, feat, w_val, b_val, w_out, b_out, ga
                 nc.sync.dma_start(out=out_rows[:, j, half], in_=result[:])
 
         def finish(j):
-            for h in range(HALVES):
-                half = slice(h * BANK, (h + 1) * BANK)
-                result = rows.tile([P, BANK], F32, bufs=4)
+            pieces = 2 if j == TILES - 1 else 1
+            width = SIZE // pieces
+            for h in range(pieces):
+                half = slice(h * width, (h + 1) * width)
+                result = rows.tile([P, width], F32, name="last" if pieces == 2 else "finished")
                 nc.vector.scalar_tensor_tensor(
                     out=result[:], in0=centred_of[j][:, half], scalar=inverse_of[j][:], in1=shift_all[:, half],
                     op0=ALU.mult, op1=ALU.add,
@@ -313,35 +322,41 @@ def tile_efficientfusionlayer_pa_kernel(tc, feat, w_val, b_val, w_out, b_out, ga
                     start=True, stop=True,
                 )
 
-        value_rounds = VALUE_ROUNDS
-        for n in range(FLIP_LEAD):
-            flip_pair(n)
+        flip_pair(0)
         quantise_pair(0)
-        previous = None
-        h = 0
+        for n in range(1, FLIP_LEAD):
+            flip_pair(n)
+        pending = []
+        half_done = []
+
+        def empty_pending():
+            while pending:
+                q = pending.pop(0)
+                value_empty(q)
+                if q % 2 == 1:
+                    half_done.append(q // 2)
+
+        def quantise_done(keep_last):
+            while len(half_done) > keep_last:
+                value_quantise(half_done.pop(0))
+
         for n in range(len(pairs) + 1):
             if n + 1 < len(pairs):
                 quantise_pair(n + 1)
-            if previous is not None:
-                value_empty(2 * previous + 1)
+            empty_pending()
             if FLIP_FIRST and n + FLIP_LEAD < len(pairs):
                 flip_pair(n + FLIP_LEAD)
-            current = None
-            if n in value_rounds:
-                current = h
-                h += 1
-                value_matmuls(2 * current)
-                value_matmuls(2 * current + 1)
+            banks_now = ROUND_BANKS.get(n, ())
+            for q in banks_now:
+                value_matmuls(q)
+                pending.append(q)
             if not FLIP_FIRST and n + FLIP_LEAD < len(pairs):
                 flip_pair(n + FLIP_LEAD)
-            if current is not None:
-                value_empty(2 * current)
-            if previous is not None:
-                value_quantise(previous)
-            previous = current
-            if n in RES_ROUNDS:
-                half = RES_ROUNDS.index(n)
-                residual_half(half // 2, half % 2)
+            if len(pending) > 1:
+                value_empty(pending.pop(0))
+            quantise_done(0)
+            for half in RES_ROUNDS.get(n, ()):
+                residual_half(RES_FIRST + half // 2, half % 2)
             if n == B_OUT_AT:
                 b_out_all = keep.tile([P, SIZE], BF16)
                 b_out_bank = psum_keep.tile([P, SIZE], BF16, name="gain_all")
@@ -349,49 +364,56 @@ def tile_efficientfusionlayer_pa_kernel(tc, feat, w_val, b_val, w_out, b_out, ga
                 nc.scalar.copy(out=b_out_all[:], in_=b_out_bank[:])
                 if scalar_banks:
                     nc.scalar.copy(out=bias_val[:], in_=bias_bf[:])
-                for j in range(RES_LEAD):
+                for j in range(RES_FIRST):
                     add_b_out(j)
-            if n == 9:
-                pass
+            if n == LATE_AT:
+                b_out_late = keep.tile([P, SIZE], BF16)
+                nc.scalar.copy(out=b_out_late[:], in_=b_out_all[:])
+                for j in range(RES_FIRST, RES_BUFS):
+                    if j not in PE_TILES:
+                        add_b_out(j)
+            if not SHIFT_PSUM and n == SHIFT_AT:
+                shift_bank = psum_wide.tile([P, SIZE], BF16, tag="wide")
+                spread(2, shift_bank)
+                shift_all_sb = keep.tile([P, SIZE], BF16)
+                nc.scalar.copy(out=shift_all_sb[:], in_=shift_bank[:])
         output_matmuls(0)
         gain_all = psum_keep.tile([P, SIZE], BF16, name="gain_all")
         spread(1, gain_all)
-        shift_all = psum_val.tile([P, SIZE], BF16, name="acc")
-        spread(2, shift_all)
-        shift_all_sb = keep.tile([P, SIZE], BF16)
-        nc.scalar.copy(out=shift_all_sb[:], in_=shift_all[:])
+        if SHIFT_PSUM:
+            shift_placed.append(True)
+            shift_all = psum_val.tile([P, SIZE], BF16, tag="spare", bufs=1)
+            spread(2, shift_all)
+            shift_all_sb = keep.tile([P, SIZE], BF16)
+            nc.scalar.copy(out=shift_all_sb[:], in_=shift_all[:])
+        else:
+            shift_all = shift_all_sb
+        for half in RES_ROUNDS.get(13, ()):
+            residual_half(RES_FIRST + half // 2, half % 2)
 
         gpsimd_tiles = GPSIMD_TILES
-        value_steps = VALUE_STEPS
         for s in range(TILES + 2):
+            for q in STEP_BANKS.get(s, ()):
+                value_matmuls(q)
+                pending.append(q)
             if s + 1 < TILES:
                 output_matmuls(s + 1)
-            current = None
-            if s in value_steps:
-                current = h
-                h += 1
-                value_matmuls(2 * current)
-                value_matmuls(2 * current + 1)
             if s < TILES:
                 add_residual(s, 0)
             if 0 <= s - 1 < TILES:
                 mean(s - 1)
                 centre(s - 1)
-            if (s - 2) in gpsimd_tiles:
-                scale_rows(s - 2)
-            if 0 <= s - 1 < TILES:
+                if not SCALE_LATE and (s - 2) in gpsimd_tiles:
+                    scale_rows(s - 2)
                 sum_of_squares(s - 1)
                 invert(s - 1)
+            empty_pending()
+            if (SCALE_LATE or s > TILES) and (s - 2) in gpsimd_tiles:
+                scale_rows(s - 2)
             if 0 <= s - 2 and not (s - 2) in gpsimd_tiles:
                 finish(s - 2)
-            if current is not None:
-                value_empty(2 * current)
             if s < TILES:
                 add_residual(s, 1)
-            if current is not None:
-                value_empty(2 * current + 1)
-            if previous is not None:
-                value_quantise(previous)
-            previous = current
-            if s + RES_LEAD < TILES:
-                add_b_out(s + RES_LEAD)
+            quantise_done(0)
+            if s + RES_BUFS < TILES and s + RES_BUFS not in PE_TILES:
+                add_b_out(s + RES_BUFS)

@@ -21,6 +21,8 @@ PAIRS = SIZE // PAIR
 BANK = 512
 HALVES = SIZE // BANK
 EPS = 1e-5
+GAIN_AT = 9
+EARLY_OUT = True
 LATE_AT = 11
 SHIFT_AT = 10
 SHIFT_PSUM = True
@@ -29,15 +31,17 @@ FLIP_LEAD = 2
 FLIP_FIRST = True
 STAGE = 5
 SCALAR_BANKS = (5, 9, 13)
-VECTOR_FLIPS = 3
-ROUND_BANKS = {2: (0, 1), 3: (2, 3), 5: (4, 5), 6: (6, 7), 7: (8, 9), 8: (10, 11), 9: (12, 13), 10: (14, 15)}
+VECTOR_FLIPS = 2
+ROUND_BANKS = {2: (0,), 3: (1, 2), 4: (3,), 5: (4, 5), 6: (6, 7), 7: (8, 9), 8: (10, 11), 9: (12, 13), 10: (14, 15)}
 STEP_BANKS = {}
 ORDER_TAIL = [("feat", 2), ("feat", 3)] + [("wo", r) for r in range(4)]
-RES_BUFS = 3
-RES_ROUNDS = {}
-PE_TILES = ()
+RES_BUFS = 4
+RES_ROUNDS = {11: (0,), 12: (1,)}
+PE_TILES = (2,)
+STEP_PE = ()
+PE_AHEAD = 2
 RES_FIRST = 2
-B_OUT_AT = 1
+B_OUT_AT = 2
 GPSIMD_TILES = (0, 2, 3, 5)
 
 FLOPS = 2 * 2 * SIZE * SIZE * SIZE
@@ -329,12 +333,15 @@ def tile_efficientfusionlayer_pa_kernel(tc, feat, w_val, b_val, w_out, b_out, ga
         pending = []
         half_done = []
 
+        def empty_next():
+            q = pending.pop(0)
+            value_empty(q)
+            if q % 2 == 1:
+                half_done.append(q // 2)
+
         def empty_pending():
             while pending:
-                q = pending.pop(0)
-                value_empty(q)
-                if q % 2 == 1:
-                    half_done.append(q // 2)
+                empty_next()
 
         def quantise_done(keep_last):
             while len(half_done) > keep_last:
@@ -353,7 +360,7 @@ def tile_efficientfusionlayer_pa_kernel(tc, feat, w_val, b_val, w_out, b_out, ga
             if not FLIP_FIRST and n + FLIP_LEAD < len(pairs):
                 flip_pair(n + FLIP_LEAD)
             if len(pending) > 1:
-                value_empty(pending.pop(0))
+                empty_next()
             quantise_done(0)
             for half in RES_ROUNDS.get(n, ()):
                 residual_half(RES_FIRST + half // 2, half % 2)
@@ -366,6 +373,9 @@ def tile_efficientfusionlayer_pa_kernel(tc, feat, w_val, b_val, w_out, b_out, ga
                     nc.scalar.copy(out=bias_val[:], in_=bias_bf[:])
                 for j in range(RES_FIRST):
                     add_b_out(j)
+            if n == GAIN_AT:
+                gain_all = psum_keep.tile([P, SIZE], BF16, name="gain_all")
+                spread(1, gain_all)
             if n == LATE_AT:
                 b_out_late = keep.tile([P, SIZE], BF16)
                 nc.scalar.copy(out=b_out_late[:], in_=b_out_all[:])
@@ -378,14 +388,15 @@ def tile_efficientfusionlayer_pa_kernel(tc, feat, w_val, b_val, w_out, b_out, ga
                 shift_all_sb = keep.tile([P, SIZE], BF16)
                 nc.scalar.copy(out=shift_all_sb[:], in_=shift_bank[:])
         output_matmuls(0)
-        gain_all = psum_keep.tile([P, SIZE], BF16, name="gain_all")
-        spread(1, gain_all)
         if SHIFT_PSUM:
             shift_placed.append(True)
             shift_all = psum_val.tile([P, SIZE], BF16, tag="spare", bufs=1)
+            if EARLY_OUT:
+                output_matmuls(1)
             spread(2, shift_all)
             shift_all_sb = keep.tile([P, SIZE], BF16)
-            nc.scalar.copy(out=shift_all_sb[:], in_=shift_all[:])
+            if not EARLY_OUT:
+                nc.scalar.copy(out=shift_all_sb[:], in_=shift_all[:])
         else:
             shift_all = shift_all_sb
         for half in RES_ROUNDS.get(13, ()):
@@ -396,7 +407,7 @@ def tile_efficientfusionlayer_pa_kernel(tc, feat, w_val, b_val, w_out, b_out, ga
             for q in STEP_BANKS.get(s, ()):
                 value_matmuls(q)
                 pending.append(q)
-            if s + 1 < TILES:
+            if s + 1 < TILES and (s > 0 or not EARLY_OUT):
                 output_matmuls(s + 1)
             if s < TILES:
                 add_residual(s, 0)
@@ -407,6 +418,8 @@ def tile_efficientfusionlayer_pa_kernel(tc, feat, w_val, b_val, w_out, b_out, ga
                     scale_rows(s - 2)
                 sum_of_squares(s - 1)
                 invert(s - 1)
+                if EARLY_OUT and s == 1:
+                    nc.scalar.copy(out=shift_all_sb[:], in_=shift_all[:])
             empty_pending()
             if (SCALE_LATE or s > TILES) and (s - 2) in gpsimd_tiles:
                 scale_rows(s - 2)
@@ -417,3 +430,6 @@ def tile_efficientfusionlayer_pa_kernel(tc, feat, w_val, b_val, w_out, b_out, ga
             quantise_done(0)
             if s + RES_BUFS < TILES and s + RES_BUFS not in PE_TILES:
                 add_b_out(s + RES_BUFS)
+            if s + PE_AHEAD in STEP_PE:
+                residual_half(s + PE_AHEAD, 0)
+                residual_half(s + PE_AHEAD, 1)

@@ -21,6 +21,7 @@ PAIRS = SIZE // PAIR
 BANK = 512
 HALVES = SIZE // BANK
 EPS = 1e-5
+LAST_PIECES = {6: 2, 7: 4}
 GAIN_AT = 9
 EARLY_OUT = True
 LATE_AT = 11
@@ -59,6 +60,10 @@ def tile_efficientfusionlayer_pa_kernel(tc, feat, w_val, b_val, w_out, b_out, ga
         psum_val = ctx.enter_context(tc.psum_pool(name="psum_val", bufs=2))
         ctx.enter_context(tc.manual_schedule())
 
+        ones = keep.tile([P, P], BF16)
+        nc.vector.memset(ones[:], 1.0)
+        idle = keep.tile([P, BANK], BF16)
+        nc.vector.memset(idle[:].bitcast(U32), 0)
         eps = keep.tile([P, 1], F32)
         nc.vector.memset(eps[:], EPS)
         bias_bf = keep.tile([P, TILES], BF16)
@@ -105,8 +110,6 @@ def tile_efficientfusionlayer_pa_kernel(tc, feat, w_val, b_val, w_out, b_out, ga
         make_identity(nc, identity[:])
         identity_bf = keep.tile([P, P], BF16)
         make_identity(nc, identity_bf[:])
-        ones = keep.tile([P, P], BF16)
-        nc.vector.memset(ones[:], 1.0)
         scalar_banks = SCALAR_BANKS
         bias_val = keep.tile([P, TILES], F32)
 
@@ -307,11 +310,11 @@ def tile_efficientfusionlayer_pa_kernel(tc, feat, w_val, b_val, w_out, b_out, ga
                 nc.sync.dma_start(out=out_rows[:, j, half], in_=result[:])
 
         def finish(j):
-            pieces = 2 if j == TILES - 1 else 1
+            pieces = LAST_PIECES.get(j, 1)
             width = SIZE // pieces
             for h in range(pieces):
                 half = slice(h * width, (h + 1) * width)
-                result = rows.tile([P, width], F32, name="last" if pieces == 2 else "finished")
+                result = rows.tile([P, width], F32, name="finished_%d" % pieces, bufs=2 * pieces)
                 nc.vector.scalar_tensor_tensor(
                     out=result[:], in0=centred_of[j][:, half], scalar=inverse_of[j][:], in1=shift_all[:, half],
                     op0=ALU.mult, op1=ALU.add,
@@ -326,9 +329,17 @@ def tile_efficientfusionlayer_pa_kernel(tc, feat, w_val, b_val, w_out, b_out, ga
                     start=True, stop=True,
                 )
 
+        warm_bank = psum_keep.tile([P, BANK], F32, name="gain_all")
+
+        def keep_warm(count):
+            for k in range(count):
+                nc.tensor.matmul(out=warm_bank[:], lhsT=ones[:], rhs=idle[:], start=True, stop=True)
+
+        keep_warm(3)
         flip_pair(0)
         quantise_pair(0)
         for n in range(1, FLIP_LEAD):
+            keep_warm(1)
             flip_pair(n)
         pending = []
         half_done = []
@@ -352,6 +363,8 @@ def tile_efficientfusionlayer_pa_kernel(tc, feat, w_val, b_val, w_out, b_out, ga
                 quantise_pair(n + 1)
             empty_pending()
             if FLIP_FIRST and n + FLIP_LEAD < len(pairs):
+                if n < 2:
+                    keep_warm(1)
                 flip_pair(n + FLIP_LEAD)
             banks_now = ROUND_BANKS.get(n, ())
             for q in banks_now:

@@ -21,6 +21,7 @@ PAIRS = SIZE // PAIR
 BANK = 512
 HALVES = SIZE // BANK
 EPS = 1e-5
+EARLY_PIECES = 4
 LAST_PIECES = {6: 2, 7: 4}
 GAIN_AT = 9
 EARLY_OUT = True
@@ -38,12 +39,12 @@ STEP_BANKS = {}
 ORDER_TAIL = [("feat", 2), ("feat", 3)] + [("wo", r) for r in range(4)]
 RES_BUFS = 4
 RES_ROUNDS = {11: (0,), 12: (1,)}
-PE_TILES = (2,)
-STEP_PE = ()
-PE_AHEAD = 2
+PE_TILES = (2, 7)
+STEP_PE = (7,)
+PE_AHEAD = 3
 RES_FIRST = 2
 B_OUT_AT = 2
-GPSIMD_TILES = (0, 2, 3, 5)
+GPSIMD_TILES = (0, 1, 3, 4, 5)
 
 FLOPS = 2 * 2 * SIZE * SIZE * SIZE
 
@@ -225,17 +226,21 @@ def tile_efficientfusionlayer_pa_kernel(tc, feat, w_val, b_val, w_out, b_out, ga
 
         def add_b_out(j):
             residual_of[j] = rows.tile([P, SIZE], F32, name="residual", bufs=RES_BUFS)
-            for h in range(HALVES):
+            width = SIZE // (EARLY_PIECES if j < RES_FIRST else HALVES)
+            for first in range(0, SIZE, width):
                 nc.gpsimd.tensor_tensor(
-                    out=residual_of[j][:, h * BANK : (h + 1) * BANK],
-                    in0=raw["feat"][:, j * SIZE + h * BANK : j * SIZE + (h + 1) * BANK],
-                    in1=(b_out_all if j < RES_FIRST else b_out_late)[:, h * BANK : (h + 1) * BANK], op=ALU.add,
+                    out=residual_of[j][:, first : first + width],
+                    in0=raw["feat"][:, j * SIZE + first : j * SIZE + first + width],
+                    in1=(b_out_all if j < RES_FIRST else b_out_late)[:, first : first + width], op=ALU.add,
                 )
 
         def residual_half(j, h):
             if h == 0:
                 residual_of[j] = rows.tile([P, SIZE], F32, name="residual", bufs=RES_BUFS)
-            bank = psum_wide.tile([P, BANK], F32, tag="wide")
+            if shift_placed:
+                bank = psum_val.tile([P, BANK], F32, tag="acc", bufs=2)
+            else:
+                bank = psum_wide.tile([P, BANK], F32, tag="wide")
             half = slice(h * BANK, (h + 1) * BANK)
             nc.tensor.matmul(
                 out=bank[:], lhsT=identity_bf[:], rhs=raw["feat"][:, j * SIZE + h * BANK : j * SIZE + (h + 1) * BANK],

@@ -21,6 +21,12 @@ PAIRS = SIZE // PAIR
 BANK = 512
 HALVES = SIZE // BANK
 EPS = 1e-5
+EMPTY_FIRST = tuple(range(12))
+VECTOR_MEANS = (7,)
+GATE_BLOCK = 7
+SPLIT_STORE = True
+KEEP_LAST = 0
+OUT0_AT = 99
 EARLY_PIECES = 4
 LAST_PIECES = {6: 2, 7: 4}
 GAIN_AT = 9
@@ -33,7 +39,7 @@ FLIP_LEAD = 2
 FLIP_FIRST = True
 STAGE = 5
 SCALAR_BANKS = (5, 9, 13)
-VECTOR_FLIPS = 2
+VECTOR_FLIPS = 0
 ROUND_BANKS = {2: (0,), 3: (1, 2), 4: (3,), 5: (4, 5), 6: (6, 7), 7: (8, 9), 8: (10, 11), 9: (12, 13), 10: (14, 15)}
 STEP_BANKS = {}
 ORDER_TAIL = [("feat", 2), ("feat", 3)] + [("wo", r) for r in range(4)]
@@ -67,6 +73,8 @@ def tile_efficientfusionlayer_pa_kernel(tc, feat, w_val, b_val, w_out, b_out, ga
         nc.vector.memset(idle[:].bitcast(U32), 0)
         eps = keep.tile([P, 1], F32)
         nc.vector.memset(eps[:], EPS)
+        minus_share = keep.tile([P, 1], F32)
+        nc.vector.memset(minus_share[:], -1.0 / SIZE)
         bias_bf = keep.tile([P, TILES], BF16)
         with nc.allow_non_contiguous_dma(reason="1024 bias values, two to a piece"):
             nc.scalar.dma_start(
@@ -217,6 +225,8 @@ def tile_efficientfusionlayer_pa_kernel(tc, feat, w_val, b_val, w_out, b_out, ga
 
         att_acc = {}
         residual_of = {}
+        tail_store = []
+        gpsimd_tiles = GPSIMD_TILES
         y_of = {}
         sums_of = {}
         minus_mean_of = {}
@@ -231,7 +241,7 @@ def tile_efficientfusionlayer_pa_kernel(tc, feat, w_val, b_val, w_out, b_out, ga
                 nc.gpsimd.tensor_tensor(
                     out=residual_of[j][:, first : first + width],
                     in0=raw["feat"][:, j * SIZE + first : j * SIZE + first + width],
-                    in1=(b_out_all if j < RES_FIRST else b_out_late)[:, first : first + width], op=ALU.add,
+                    in1=b_out_all[:, first : first + width], op=ALU.add,
                 )
 
         def residual_half(j, h):
@@ -275,6 +285,12 @@ def tile_efficientfusionlayer_pa_kernel(tc, feat, w_val, b_val, w_out, b_out, ga
 
         def mean(j):
             minus_mean_of[j] = stats.tile([P, 1], F32, name="minus_mean")
+            if j in VECTOR_MEANS:
+                nc.vector.scalar_tensor_tensor(
+                    out=minus_mean_of[j][:], in0=sums_of[j][:, 0:1], scalar=sums_of[j][:, 1:2], in1=minus_share[:],
+                    op0=ALU.add, op1=ALU.mult,
+                )
+                return
             shares = stats.tile([P, HALVES], F32)
             nc.scalar.activation(
                 out=shares[:], in_=sums_of[j][:], func=ACT.Identity, scale=-1.0 / SIZE,
@@ -312,7 +328,10 @@ def tile_efficientfusionlayer_pa_kernel(tc, feat, w_val, b_val, w_out, b_out, ga
                 half = slice(h * BANK, (h + 1) * BANK)
                 result = rows.tile([P, BANK], F32, bufs=4)
                 nc.gpsimd.tensor_tensor(out=result[:], in0=scaled[:, half], in1=shift_all_sb[:, half], op=ALU.add)
-                nc.sync.dma_start(out=out_rows[:, j, half], in_=result[:])
+                if (j, h) == (max(gpsimd_tiles), 1) and SPLIT_STORE:
+                    tail_store.append((j, half, result))
+                else:
+                    nc.sync.dma_start(out=out_rows[:, j, half], in_=result[:])
 
         def finish(j):
             pieces = LAST_PIECES.get(j, 1)
@@ -364,6 +383,8 @@ def tile_efficientfusionlayer_pa_kernel(tc, feat, w_val, b_val, w_out, b_out, ga
                 value_quantise(half_done.pop(0))
 
         for n in range(len(pairs) + 1):
+            if n in EMPTY_FIRST:
+                empty_pending()
             if n + 1 < len(pairs):
                 quantise_pair(n + 1)
             empty_pending()
@@ -379,7 +400,9 @@ def tile_efficientfusionlayer_pa_kernel(tc, feat, w_val, b_val, w_out, b_out, ga
                 flip_pair(n + FLIP_LEAD)
             if len(pending) > 1:
                 empty_next()
-            quantise_done(0)
+            quantise_done(KEEP_LAST)
+            if n == OUT0_AT:
+                output_matmuls(0)
             for half in RES_ROUNDS.get(n, ()):
                 residual_half(RES_FIRST + half // 2, half % 2)
             if n == B_OUT_AT:
@@ -395,8 +418,9 @@ def tile_efficientfusionlayer_pa_kernel(tc, feat, w_val, b_val, w_out, b_out, ga
                 gain_all = psum_keep.tile([P, SIZE], BF16, name="gain_all")
                 spread(1, gain_all)
             if n == LATE_AT:
-                b_out_late = keep.tile([P, SIZE], BF16)
-                nc.scalar.copy(out=b_out_late[:], in_=b_out_all[:])
+                if GATE_BLOCK is not None:
+                    gate = keep.tile([P, 2], BF16)
+                    nc.gpsimd.tensor_copy(out=gate[:], in_=packed_of[GATE_BLOCK][:, 0:2])
                 for j in range(RES_FIRST, RES_BUFS):
                     if j not in PE_TILES:
                         add_b_out(j)
@@ -405,7 +429,8 @@ def tile_efficientfusionlayer_pa_kernel(tc, feat, w_val, b_val, w_out, b_out, ga
                 spread(2, shift_bank)
                 shift_all_sb = keep.tile([P, SIZE], BF16)
                 nc.scalar.copy(out=shift_all_sb[:], in_=shift_bank[:])
-        output_matmuls(0)
+        if OUT0_AT > len(pairs):
+            output_matmuls(0)
         if SHIFT_PSUM:
             shift_placed.append(True)
             shift_all = psum_val.tile([P, SIZE], BF16, tag="spare", bufs=1)
@@ -420,7 +445,6 @@ def tile_efficientfusionlayer_pa_kernel(tc, feat, w_val, b_val, w_out, b_out, ga
         for half in RES_ROUNDS.get(13, ()):
             residual_half(RES_FIRST + half // 2, half % 2)
 
-        gpsimd_tiles = GPSIMD_TILES
         for s in range(TILES + 2):
             for q in STEP_BANKS.get(s, ()):
                 value_matmuls(q)
@@ -438,6 +462,9 @@ def tile_efficientfusionlayer_pa_kernel(tc, feat, w_val, b_val, w_out, b_out, ga
                 invert(s - 1)
                 if EARLY_OUT and s == 1:
                     nc.scalar.copy(out=shift_all_sb[:], in_=shift_all[:])
+            if s == TILES:
+                for j, half, result in tail_store:
+                    nc.scalar.dma_start(out=out_rows[:, j, half], in_=result[:])
             empty_pending()
             if (SCALE_LATE or s > TILES) and (s - 2) in gpsimd_tiles:
                 scale_rows(s - 2)

@@ -21,6 +21,7 @@ PAIRS = SIZE // PAIR
 BANK = 512
 HALVES = SIZE // BANK
 EPS = 1e-5
+LATE_PIECES = 2
 EMPTY_FIRST = tuple(range(12))
 VECTOR_MEANS = (7,)
 GATE_BLOCK = 7
@@ -75,12 +76,9 @@ def tile_efficientfusionlayer_pa_kernel(tc, feat, w_val, b_val, w_out, b_out, ga
         nc.vector.memset(eps[:], EPS)
         minus_share = keep.tile([P, 1], F32)
         nc.vector.memset(minus_share[:], -1.0 / SIZE)
-        bias_bf = keep.tile([P, TILES], BF16)
-        with nc.allow_non_contiguous_dma(reason="1024 bias values, two to a piece"):
-            nc.scalar.dma_start(
-                out=bias_bf[:].rearrange("p (r e) -> p r e", e=2),
-                in_=b_val.rearrange("(r p e) -> p r e", p=P, e=2),
-            )
+        bias_rows = keep.tile([P, PAIR], BF16)
+        nc.vector.memset(bias_rows[:].bitcast(U32), 0)
+        nc.scalar.dma_start(out=bias_rows[0:PAIRS, :], in_=b_val.rearrange("(r q) -> r q", r=PAIRS))
         warm = keep.tile([P, 1], F32)
         nc.scalar.activation(out=warm[:], in_=eps[:], func=ACT.Abs_reciprocal_sqrt)
         vectors = keep.tile([P, 3 * SIZE], BF16)
@@ -236,7 +234,7 @@ def tile_efficientfusionlayer_pa_kernel(tc, feat, w_val, b_val, w_out, b_out, ga
 
         def add_b_out(j):
             residual_of[j] = rows.tile([P, SIZE], F32, name="residual", bufs=RES_BUFS)
-            width = SIZE // (EARLY_PIECES if j < RES_FIRST else HALVES)
+            width = SIZE // (EARLY_PIECES if j < RES_FIRST else LATE_PIECES)
             for first in range(0, SIZE, width):
                 nc.gpsimd.tensor_tensor(
                     out=residual_of[j][:, first : first + width],
@@ -403,6 +401,11 @@ def tile_efficientfusionlayer_pa_kernel(tc, feat, w_val, b_val, w_out, b_out, ga
             quantise_done(KEEP_LAST)
             if n == OUT0_AT:
                 output_matmuls(0)
+            if n == 0:
+                bias_bank = psum_wide.tile([P, P], F32, tag="wide")
+                nc.tensor.transpose(bias_bank[:], bias_rows[:].bitcast(F32), identity[:])
+                bias_bf = keep.tile([P, TILES], BF16)
+                nc.vector.tensor_copy(out=bias_bf[:].bitcast(F32), in_=bias_bank[:, 0:PAIRS])
             for half in RES_ROUNDS.get(n, ()):
                 residual_half(RES_FIRST + half // 2, half % 2)
             if n == B_OUT_AT:

@@ -21,6 +21,9 @@ PAIRS = SIZE // PAIR
 BANK = 512
 HALVES = SIZE // BANK
 EPS = 1e-5
+SHIFT_PIECES = 1
+WARM = (512, 256)
+WARM_ROUNDS = 2
 LATE_PIECES = 2
 EMPTY_FIRST = tuple(range(12))
 VECTOR_MEANS = (7,)
@@ -322,9 +325,10 @@ def tile_efficientfusionlayer_pa_kernel(tc, feat, w_val, b_val, w_out, b_out, ga
             nc.scalar.activation(
                 out=scaled[:], in_=centred_of[j][:], func=ACT.Copy, scale=inverse_of[j][:],
             )
-            for h in range(HALVES):
-                half = slice(h * BANK, (h + 1) * BANK)
-                result = rows.tile([P, BANK], F32, bufs=4)
+            pieces = HALVES if j == max(gpsimd_tiles) else SHIFT_PIECES
+            for h in range(pieces):
+                half = slice(h * SIZE // pieces, (h + 1) * SIZE // pieces)
+                result = rows.tile([P, SIZE // pieces], F32, name="shifted_%d" % pieces, bufs=2)
                 nc.gpsimd.tensor_tensor(out=result[:], in0=scaled[:, half], in1=shift_all_sb[:, half], op=ALU.add)
                 if (j, h) == (max(gpsimd_tiles), 1) and SPLIT_STORE:
                     tail_store.append((j, half, result))
@@ -353,15 +357,17 @@ def tile_efficientfusionlayer_pa_kernel(tc, feat, w_val, b_val, w_out, b_out, ga
 
         warm_bank = psum_keep.tile([P, BANK], F32, name="gain_all")
 
-        def keep_warm(count):
-            for k in range(count):
-                nc.tensor.matmul(out=warm_bank[:], lhsT=ones[:], rhs=idle[:], start=True, stop=True)
+        def keep_warm(*widths):
+            for width in widths:
+                nc.tensor.matmul(
+                    out=warm_bank[:, 0:width], lhsT=ones[:], rhs=idle[:, 0:width], start=True, stop=True
+                )
 
-        keep_warm(3)
+        keep_warm(BANK, BANK, BANK)
         flip_pair(0)
         quantise_pair(0)
         for n in range(1, FLIP_LEAD):
-            keep_warm(1)
+            keep_warm(*WARM)
             flip_pair(n)
         pending = []
         half_done = []
@@ -387,8 +393,8 @@ def tile_efficientfusionlayer_pa_kernel(tc, feat, w_val, b_val, w_out, b_out, ga
                 quantise_pair(n + 1)
             empty_pending()
             if FLIP_FIRST and n + FLIP_LEAD < len(pairs):
-                if n < 2:
-                    keep_warm(1)
+                if n < WARM_ROUNDS:
+                    keep_warm(*WARM)
                 flip_pair(n + FLIP_LEAD)
             banks_now = ROUND_BANKS.get(n, ())
             for q in banks_now:

from contextlib import ExitStack

import concourse.mybir as mybir
from concourse.masks import make_identity

F32 = mybir.dt.float32
BF16 = mybir.dt.bfloat16
U32 = mybir.dt.uint32
U8 = mybir.dt.uint8
FP8X4 = mybir.dt.float8_e4m3fn_x4
ACT = mybir.ActivationFunctionType
ALU = mybir.AluOpType

P = 128
PACK = 4
SIZE = 1024
PASSES = SIZE // (P * PACK)
TILES = SIZE // P
PAIR = 2 * P
PAIRS = SIZE // PAIR
BANK = 512
HALVES = SIZE // BANK
EPS = 1e-5
SHIFT_PIECES = 1
WARM = (512, 256)
WARM_ROUNDS = 2
LATE_PIECES = 2
EMPTY_FIRST = tuple(range(12))
VECTOR_MEANS = (7,)
GATE_BLOCK = 7
SPLIT_STORE = True
KEEP_LAST = 0
OUT0_AT = 99
EARLY_PIECES = 4
LAST_PIECES = {6: 2, 7: 4}
GAIN_AT = 9
EARLY_OUT = True
LATE_AT = 11
SHIFT_AT = 10
SHIFT_PSUM = True
SCALE_LATE = False
FLIP_LEAD = 2
FLIP_FIRST = True
STAGE = 5
SCALAR_BANKS = (5, 9, 13)
VECTOR_FLIPS = 0
ROUND_BANKS = {2: (0,), 3: (1, 2), 4: (3,), 5: (4, 5), 6: (6, 7), 7: (8, 9), 8: (10, 11), 9: (12, 13), 10: (14, 15)}
STEP_BANKS = {}
ORDER_TAIL = [("feat", 2), ("feat", 3)] + [("wo", r) for r in range(4)]
RES_BUFS = 4
RES_ROUNDS = {11: (0,), 12: (1,)}
PE_TILES = (2, 7)
STEP_PE = (7,)
PE_AHEAD = 3
RES_FIRST = 2
B_OUT_AT = 2
GPSIMD_TILES = (0, 1, 3, 4, 5)

FLOPS = 2 * 2 * SIZE * SIZE * SIZE


def tile_efficientfusionlayer_pa_kernel(tc, feat, w_val, b_val, w_out, b_out, gain, shift, out):
    nc = tc.nc
    with ExitStack() as ctx:
        keep = ctx.enter_context(tc.tile_pool(name="keep", bufs=1))
        stage = ctx.enter_context(tc.tile_pool(name="stage", bufs=STAGE))
        rows = ctx.enter_context(tc.tile_pool(name="rows", bufs=2))
        stats = ctx.enter_context(tc.tile_pool(name="stats", bufs=3))
        psum_keep = ctx.enter_context(tc.psum_pool(name="psum_keep", bufs=1))
        psum_wide = ctx.enter_context(tc.psum_pool(name="psum_wide", bufs=4))
        psum_val = ctx.enter_context(tc.psum_pool(name="psum_val", bufs=2))
        ctx.enter_context(tc.manual_schedule())

        ones = keep.tile([P, P], BF16)
        nc.vector.memset(ones[:], 1.0)
        idle = keep.tile([P, BANK], BF16)
        nc.vector.memset(idle[:].bitcast(U32), 0)
        eps = keep.tile([P, 1], F32)
        nc.vector.memset(eps[:], EPS)
        minus_share = keep.tile([P, 1], F32)
        nc.vector.memset(minus_share[:], -1.0 / SIZE)
        bias_rows = keep.tile([P, PAIR], BF16)
        nc.vector.memset(bias_rows[:].bitcast(U32), 0)
        nc.scalar.dma_start(out=bias_rows[0:PAIRS, :], in_=b_val.rearrange("(r q) -> r q", r=PAIRS))
        warm = keep.tile([P, 1], F32)
        nc.scalar.activation(out=warm[:], in_=eps[:], func=ACT.Abs_reciprocal_sqrt)
        vectors = keep.tile([P, 3 * SIZE], BF16)
        nc.vector.memset(vectors[:].bitcast(U32), 0)
        for v, vector in enumerate((b_out, gain, shift)):
            nc.scalar.dma_start(
                out=vectors[0:1, v * SIZE : (v + 1) * SIZE], in_=vector.rearrange("(o d) -> o d", o=1)
            )


        span = 2 * SIZE
        raw = {}
        for name in ("wv", "feat", "wo"):
            raw[name] = keep.tile([P, TILES * SIZE], BF16, name="raw_" + name)
        wv_rows = w_val.rearrange("(r p e) d -> p r (e d)", p=P, e=2)
        feat_rows = feat.rearrange("(p j) d -> p (j d)", j=TILES)
        wo_rows = w_out.rearrange("(i p) k -> p i k", p=P)
        pairs = [("feat", 0), ("wv", 0), ("wv", 1), ("feat", 1), ("wv", 2), ("wv", 3)]
        pairs += ORDER_TAIL
        for name, r in pairs:
            here = raw[name][:, r * span : (r + 1) * span]
            if name == "wv":
                nc.sync.dma_start(out=here, in_=wv_rows[:, r, :])
            elif name == "feat":
                pieces = 2 if r == 0 else 1
                width = span // pieces
                for first in range(r * span, (r + 1) * span, width):
                    nc.sync.dma_start(
                        out=raw[name][:, first : first + width], in_=feat_rows[:, first : first + width]
                    )
            else:
                nc.sync.dma_start(out=here.rearrange("p (i k) -> p i k", i=2), in_=wo_rows[:, 2 * r : 2 * r + 2, :])
        out_rows = out.rearrange("(p j) d -> p j d", j=TILES)

        identity = keep.tile([P, P], F32)
        make_identity(nc, identity[:])
        identity_bf = keep.tile([P, P], BF16)
        make_identity(nc, identity_bf[:])
        scalar_banks = SCALAR_BANKS
        bias_val = keep.tile([P, TILES], F32)

        codes = {}
        scales = {}
        for name in ("wv", "feat", "wo", "val"):
            codes[name] = keep.tile([P, PAIRS, PASSES, PAIR], U32, name="codes_" + name, align_bytes=64)
            scales[name] = keep.tile([P, PAIRS, PASSES, PAIR], U8, name="scales_" + name, align_bytes=64)

        grouped_of = {}

        def flip_pair(n):
            name, r = pairs[n]
            words = raw[name][:].bitcast(F32)
            grouped = stage.tile([P, PASSES * PAIR * PACK], BF16, align_bytes=64)
            grouped_words = grouped[:].bitcast(F32).rearrange("p (c n u) -> p c n u", c=PASSES, u=2)
            for i in range(2):
                flipped = psum_wide.tile([P, 2 * PASSES, P], F32, tag="wide")
                for block in range(2 * PASSES):
                    first = ((2 * r + i) * 2 * PASSES + block) * P
                    nc.tensor.transpose(flipped[:, block, :], words[:, first : first + P], identity[:])
                copy_out = nc.vector.tensor_copy if (n < VECTOR_FLIPS and i == 1) else nc.scalar.copy
                copy_out(
                    out=grouped_words[:, :, i * P : (i + 1) * P, :],
                    in_=flipped[:].rearrange("p (c u) r -> p c r u", u=2),
                )
            grouped_of[n] = grouped

        def quantise_pair(n):
            name, r = pairs[n]
            nc.vector.quantize_mx(
                out=codes[name][:, r].rearrange("p c n -> p (c n)").bitcast(FP8X4),
                scales=scales[name][:, r].rearrange("p c n -> p (c n)"),
                in_=grouped_of[n][:],
            )

        blocks = [(0, 0), (1, 0), (0, 1), (1, 1), (2, 0), (2, 1), (3, 0), (3, 1)]
        val_acc = {}
        shift_placed = []
        planes_of = {}
        packed_of = {}

        def tile_of(name, j, c):
            cols = slice((j % 2) * P, (j % 2 + 1) * P)
            return codes[name][:, j // 2, c, cols].bitcast(FP8X4), scales[name][:, j // 2, c, cols]

        def value_matmuls(q):
            r, c_val = blocks[q // 2]
            spare = q % 3 == 2 and not shift_placed
            acc = psum_val.tile([P, PACK, P], F32, tag="spare" if spare else "acc", bufs=1 if spare else 2)
            for t in range(PACK):
                for c in range(PASSES):
                    lhsT, lhsT_scale = tile_of("wv", PACK * c_val + t, c)
                    rhs, rhs_scale = tile_of("feat", 2 * r + q % 2, c)
                    nc.tensor.matmul_mx(
                        out=acc[:, t, :], lhsT=lhsT, lhsT_scale=lhsT_scale, rhs=rhs, rhs_scale=rhs_scale,
                        start=(c == 0), stop=(c == PASSES - 1),
                    )
            val_acc[q] = acc

        def value_bias(q):
            if q % 2 == 0:
                packed_of[q // 2] = stage.tile([P, PAIR * PACK], BF16, name="packed", align_bytes=64)
            first = (q % 2) * P * PACK
            c_val = blocks[q // 2][1]
            nc.vector.tensor_tensor(
                out=packed_of[q // 2][:, first : first + P * PACK].rearrange("p (n t) -> p n t", t=PACK),
                in0=val_acc[q][:].rearrange("p t n -> p n t"),
                in1=bias_bf[:, c_val * PACK : (c_val + 1) * PACK].unsqueeze(1).to_broadcast([P, P, PACK]),
                op=ALU.add,
            )

        def value_bias_on_scalar(q):
            c_val = blocks[q // 2][1]
            planes_of[q] = stage.tile([P, PACK, P], BF16, name="planes")
            for t in range(PACK):
                m = c_val * PACK + t
                nc.scalar.activation(
                    out=planes_of[q][:, t, :], in_=val_acc[q][:, t, :], func=ACT.Identity,
                    bias=bias_val[:, m : m + 1], scale=1.0,
                )

        def value_pack(q):
            if q % 2 == 0:
                packed_of[q // 2] = stage.tile([P, PAIR * PACK], BF16, name="packed", align_bytes=64)
            first = (q % 2) * P * PACK
            nc.scalar.copy(
                out=packed_of[q // 2][:, first : first + P * PACK].rearrange("p (n i t) -> p n t i", i=4, t=PACK),
                in_=planes_of[q][:].rearrange("p t (n i) -> p n t i", i=4),
            )

        def value_quantise(h):
            r, c_val = blocks[h]
            nc.vector.quantize_mx(
                out=codes["val"][:, r, c_val].bitcast(FP8X4), scales=scales["val"][:, r, c_val], in_=packed_of[h][:],
            )

        def value_empty(q):
            if q in scalar_banks:
                value_bias_on_scalar(q)
                value_pack(q)
            else:
                value_bias(q)

        att_acc = {}
        residual_of = {}
        tail_store = []
        gpsimd_tiles = GPSIMD_TILES
        y_of = {}
        sums_of = {}
        minus_mean_of = {}
        sum_squares_of = {}
        inverse_of = {}
        centred_of = {}

        def add_b_out(j):
            residual_of[j] = rows.tile([P, SIZE], F32, name="residual", bufs=RES_BUFS)
            width = SIZE // (EARLY_PIECES if j < RES_FIRST else LATE_PIECES)
            for first in range(0, SIZE, width):
                nc.gpsimd.tensor_tensor(
                    out=residual_of[j][:, first : first + width],
                    in0=raw["feat"][:, j * SIZE + first : j * SIZE + first + width],
                    in1=b_out_all[:, first : first + width], op=ALU.add,
                )

        def residual_half(j, h):
            if h == 0:
                residual_of[j] = rows.tile([P, SIZE], F32, name="residual", bufs=RES_BUFS)
            if shift_placed:
                bank = psum_val.tile([P, BANK], F32, tag="acc", bufs=2)
            else:
                bank = psum_wide.tile([P, BANK], F32, tag="wide")
            half = slice(h * BANK, (h + 1) * BANK)
            nc.tensor.matmul(
                out=bank[:], lhsT=identity_bf[:], rhs=raw["feat"][:, j * SIZE + h * BANK : j * SIZE + (h + 1) * BANK],
                start=True, stop=False,
            )
            nc.tensor.matmul(out=bank[:], lhsT=ones[:], rhs=vectors[:, half], start=False, stop=True)
            nc.scalar.copy(out=residual_of[j][:, half], in_=bank[:])

        def output_matmuls(j):
            for h in range(HALVES):
                acc = psum_wide.tile([P, BANK], F32, tag="wide")
                for i in range(2):
                    r = 2 * h + i
                    for c in range(PASSES):
                        lhsT, lhsT_scale = tile_of("val", j, c)
                        nc.tensor.matmul_mx(
                            out=acc[:, i * PAIR : (i + 1) * PAIR], lhsT=lhsT, lhsT_scale=lhsT_scale,
                            rhs=codes["wo"][:, r, c].bitcast(FP8X4), rhs_scale=scales["wo"][:, r, c],
                            start=(c == 0), stop=(c == PASSES - 1),
                        )
                att_acc[j, h] = acc

        def add_residual(j, h):
            if h == 0:
                y_of[j] = rows.tile([P, SIZE], F32, name="y", bufs=3)
                sums_of[j] = stats.tile([P, HALVES], F32, name="sums")
            nc.vector.scalar_tensor_tensor(
                out=y_of[j][:, h * BANK : (h + 1) * BANK], in0=att_acc[j, h][:], scalar=1.0,
                in1=residual_of[j][:, h * BANK : (h + 1) * BANK],
                op0=ALU.mult, op1=ALU.add, accum_out=sums_of[j][:, h : h + 1],
            )

        def mean(j):
            minus_mean_of[j] = stats.tile([P, 1], F32, name="minus_mean")
            if j in VECTOR_MEANS:
                nc.vector.scalar_tensor_tensor(
                    out=minus_mean_of[j][:], in0=sums_of[j][:, 0:1], scalar=sums_of[j][:, 1:2], in1=minus_share[:],
                    op0=ALU.add, op1=ALU.mult,
                )
                return
            shares = stats.tile([P, HALVES], F32)
            nc.scalar.activation(
                out=shares[:], in_=sums_of[j][:], func=ACT.Identity, scale=-1.0 / SIZE,
                accum_out=minus_mean_of[j][:],
            )

        def sum_of_squares(j):
            squares = rows.tile([P, SIZE], BF16)
            sum_squares_of[j] = stats.tile([P, 1], F32, name="sum_squares")
            nc.scalar.activation(
                out=squares[:], in_=y_of[j][:], func=ACT.Square, bias=minus_mean_of[j][:], scale=1.0,
                accum_out=sum_squares_of[j][:],
            )

        def invert(j):
            inverse_of[j] = stats.tile([P, 1], F32, name="inverse")
            nc.scalar.activation(
                out=inverse_of[j][:], in_=sum_squares_of[j][:], func=ACT.Abs_reciprocal_sqrt, bias=eps[:],
                scale=1.0 / SIZE,
            )

        def centre(j):
            centred_of[j] = rows.tile([P, SIZE], F32, name="centred", bufs=3)
            nc.vector.scalar_tensor_tensor(
                out=centred_of[j][:], in0=y_of[j][:], scalar=minus_mean_of[j][:], in1=gain_all[:],
                op0=ALU.add, op1=ALU.mult,
            )

        def scale_rows(j):
            scaled = rows.tile([P, SIZE], F32, bufs=3)
            nc.scalar.activation(
                out=scaled[:], in_=centred_of[j][:], func=ACT.Copy, scale=inverse_of[j][:],
            )
            pieces = HALVES if j == max(gpsimd_tiles) else SHIFT_PIECES
            for h in range(pieces):
                half = slice(h * SIZE // pieces, (h + 1) * SIZE // pieces)
                result = rows.tile([P, SIZE // pieces], F32, name="shifted_%d" % pieces, bufs=2)
                nc.gpsimd.tensor_tensor(out=result[:], in0=scaled[:, half], in1=shift_all_sb[:, half], op=ALU.add)
                if (j, h) == (max(gpsimd_tiles), 1) and SPLIT_STORE:
                    tail_store.append((j, half, result))
                else:
                    nc.sync.dma_start(out=out_rows[:, j, half], in_=result[:])

        def finish(j):
            pieces = LAST_PIECES.get(j, 1)
            width = SIZE // pieces
            for h in range(pieces):
                half = slice(h * width, (h + 1) * width)
                result = rows.tile([P, width], F32, name="finished_%d" % pieces, bufs=2 * pieces)
                nc.vector.scalar_tensor_tensor(
                    out=result[:], in0=centred_of[j][:, half], scalar=inverse_of[j][:], in1=shift_all[:, half],
                    op0=ALU.mult, op1=ALU.add,
                )
                nc.sync.dma_start(out=out_rows[:, j, half], in_=result[:])

        def spread(v, bank):
            for h in range(HALVES):
                first = v * SIZE + h * BANK
                nc.tensor.matmul(
                    out=bank[:, h * BANK : (h + 1) * BANK], lhsT=ones[:], rhs=vectors[:, first : first + BANK],
                    start=True, stop=True,
                )

        warm_bank = psum_keep.tile([P, BANK], F32, name="gain_all")

        def keep_warm(*widths):
            for width in widths:
                nc.tensor.matmul(
                    out=warm_bank[:, 0:width], lhsT=ones[:], rhs=idle[:, 0:width], start=True, stop=True
                )

        keep_warm(BANK, BANK, BANK)
        flip_pair(0)
        quantise_pair(0)
        for n in range(1, FLIP_LEAD):
            keep_warm(*WARM)
            flip_pair(n)
        pending = []
        half_done = []

        def empty_next():
            q = pending.pop(0)
            value_empty(q)
            if q % 2 == 1:
                half_done.append(q // 2)

        def empty_pending():
            while pending:
                empty_next()

        def quantise_done(keep_last):
            while len(half_done) > keep_last:
                value_quantise(half_done.pop(0))

        for n in range(len(pairs) + 1):
            if n in EMPTY_FIRST:
                empty_pending()
            if n + 1 < len(pairs):
                quantise_pair(n + 1)
            empty_pending()
            if FLIP_FIRST and n + FLIP_LEAD < len(pairs):
                if n < WARM_ROUNDS:
                    keep_warm(*WARM)
                flip_pair(n + FLIP_LEAD)
            banks_now = ROUND_BANKS.get(n, ())
            for q in banks_now:
                value_matmuls(q)
                pending.append(q)
            if not FLIP_FIRST and n + FLIP_LEAD < len(pairs):
                flip_pair(n + FLIP_LEAD)
            if len(pending) > 1:
                empty_next()
            quantise_done(KEEP_LAST)
            if n == OUT0_AT:
                output_matmuls(0)
            if n == 0:
                bias_bank = psum_wide.tile([P, P], F32, tag="wide")
                nc.tensor.transpose(bias_bank[:], bias_rows[:].bitcast(F32), identity[:])
                bias_bf = keep.tile([P, TILES], BF16)
                nc.vector.tensor_copy(out=bias_bf[:].bitcast(F32), in_=bias_bank[:, 0:PAIRS])
            for half in RES_ROUNDS.get(n, ()):
                residual_half(RES_FIRST + half // 2, half % 2)
            if n == B_OUT_AT:
                b_out_all = keep.tile([P, SIZE], BF16)
                b_out_bank = psum_keep.tile([P, SIZE], BF16, name="gain_all")
                spread(0, b_out_bank)
                nc.scalar.copy(out=b_out_all[:], in_=b_out_bank[:])
                if scalar_banks:
                    nc.scalar.copy(out=bias_val[:], in_=bias_bf[:])
                for j in range(RES_FIRST):
                    add_b_out(j)
            if n == GAIN_AT:
                gain_all = psum_keep.tile([P, SIZE], BF16, name="gain_all")
                spread(1, gain_all)
            if n == LATE_AT:
                if GATE_BLOCK is not None:
                    gate = keep.tile([P, 2], BF16)
                    nc.gpsimd.tensor_copy(out=gate[:], in_=packed_of[GATE_BLOCK][:, 0:2])
                for j in range(RES_FIRST, RES_BUFS):
                    if j not in PE_TILES:
                        add_b_out(j)
            if not SHIFT_PSUM and n == SHIFT_AT:
                shift_bank = psum_wide.tile([P, SIZE], BF16, tag="wide")
                spread(2, shift_bank)
                shift_all_sb = keep.tile([P, SIZE], BF16)
                nc.scalar.copy(out=shift_all_sb[:], in_=shift_bank[:])
        if OUT0_AT > len(pairs):
            output_matmuls(0)
        if SHIFT_PSUM:
            shift_placed.append(True)
            shift_all = psum_val.tile([P, SIZE], BF16, tag="spare", bufs=1)
            if EARLY_OUT:
                output_matmuls(1)
            spread(2, shift_all)
            shift_all_sb = keep.tile([P, SIZE], BF16)
            if not EARLY_OUT:
                nc.scalar.copy(out=shift_all_sb[:], in_=shift_all[:])
        else:
            shift_all = shift_all_sb
        for half in RES_ROUNDS.get(13, ()):
            residual_half(RES_FIRST + half // 2, half % 2)

        for s in range(TILES + 2):
            for q in STEP_BANKS.get(s, ()):
                value_matmuls(q)
                pending.append(q)
            if s + 1 < TILES and (s > 0 or not EARLY_OUT):
                output_matmuls(s + 1)
            if s < TILES:
                add_residual(s, 0)
            if 0 <= s - 1 < TILES:
                mean(s - 1)
                centre(s - 1)
                if not SCALE_LATE and (s - 2) in gpsimd_tiles:
                    scale_rows(s - 2)
                sum_of_squares(s - 1)
                invert(s - 1)
                if EARLY_OUT and s == 1:
                    nc.scalar.copy(out=shift_all_sb[:], in_=shift_all[:])
            if s == TILES:
                for j, half, result in tail_store:
                    nc.scalar.dma_start(out=out_rows[:, j, half], in_=result[:])
            empty_pending()
            if (SCALE_LATE or s > TILES) and (s - 2) in gpsimd_tiles:
                scale_rows(s - 2)
            if 0 <= s - 2 and not (s - 2) in gpsimd_tiles:
                finish(s - 2)
            if s < TILES:
                add_residual(s, 1)
            quantise_done(0)
            if s + RES_BUFS < TILES and s + RES_BUFS not in PE_TILES:
                add_b_out(s + RES_BUFS)
            if s + PE_AHEAD in STEP_PE:
                residual_half(s + PE_AHEAD, 0)
                residual_half(s + PE_AHEAD, 1)
